import numpy as np
import ml_dtypes


def mxq(x, axis, fmt="e4m3"):
    dtype, down = {"e4m3": (ml_dtypes.float8_e4m3fn, 7), "e5m2": (ml_dtypes.float8_e5m2, 14)}[fmt]
    v = np.moveaxis(np.asarray(x, np.float32).astype(ml_dtypes.bfloat16).astype(np.float64), axis, -1)
    blocks = v.reshape(v.shape[:-1] + (-1, 32))
    amax = np.abs(blocks).max(-1, keepdims=True)
    byte = np.maximum(np.where(amax > 0, np.frexp(amax)[1] - 1 + 127, 0) - down, 1)
    scale = np.exp2(byte - 127.0)
    codes = (blocks / scale).astype(np.float32).astype(dtype).astype(np.float64)
    return np.moveaxis((codes * scale).reshape(v.shape), -1, axis)


WIDE = False


def mx_kscale(k):
    if not WIDE:
        return np.ones(k)
    levels = np.array([20, -20, 10, -10, 0])
    a = np.random.permutation(np.resize(levels, k // 512 * 4)).reshape(k // 512, 4)
    idx = np.arange(k)
    return np.exp2(a[idx // 512, idx % 128 // 32])


BF16 = ml_dtypes.bfloat16


def bf(x):
    return np.asarray(x, np.float32).astype(BF16)


def f64(x):
    return np.asarray(x).astype(np.float64)


C, I, T, R, D = 8, 8, 128, 512, 256


def sigmoid(v):
    return 1.0 / (1.0 + np.exp(-v))


def setup_inputs():
    s = mx_kscale(D + D)[:D // 2]
    u = np.concatenate([np.ones(D // 2), np.minimum(s, 1.0 / s)])
    query = bf(np.random.standard_normal((C, I, T, D)) * 0.5)
    wc = bf(np.random.standard_normal((C, I, T, D)) * 6.0 / np.sqrt(R))
    w_lin0 = bf(np.random.standard_normal((D + D, D)) * 1.5 / np.sqrt(D))
    b_lin = bf(np.random.standard_normal(D) * 0.2)
    w_gate0 = bf(np.random.standard_normal((D + D, D)) * 1.5 / np.sqrt(D))
    b_gate = bf(np.random.standard_normal(D) * 0.2)
    g = bf(np.random.standard_normal((C, I, T, D)) * np.exp2(np.random.randint(-12, 1, (C, I, T, 1))) * 4.0 * u)
    cat = np.concatenate([f64(query), f64(wc)], axis=-1)
    upd = np.tanh(cat @ f64(w_lin0) + f64(b_lin))
    gate = sigmoid(cat @ f64(w_gate0) + f64(b_gate))
    return {"query": query, "wc": wc,
            "w_lin": bf(f64(w_lin0) / u), "b_lin": b_lin,
            "w_gate": bf(f64(w_gate0) / u), "b_gate": b_gate,
            "upd": np.asarray(upd, np.float32), "gate": np.asarray(gate, np.float32),
            "grad_out": g}


def reference(query, wc, w_lin, b_lin, w_gate, b_gate, upd, gate, grad_out):
    q, h, a, g = f64(query), f64(upd), f64(gate), f64(grad_out)
    dl = g * (1.0 - a) * (1.0 - h * h)
    dg = g * (q - h) * a * (1.0 - a)
    dz = np.concatenate([dl, dg], axis=-1)
    w = np.concatenate([f64(w_lin)[:D], f64(w_gate)[:D]], axis=1)
    return g * a + (mxq(dz, 3, "e5m2") @ mxq(w, 1, "e4m3").T)

@@ -1,0 +1,185 @@
+from contextlib import ExitStack
+
+import concourse.mybir as mybir
+from concourse.masks import make_identity
+
+F32 = mybir.dt.float32
+BF16 = mybir.dt.bfloat16
+U32 = mybir.dt.uint32
+U8 = mybir.dt.uint8
+I32 = mybir.dt.int32
+E5M2X4 = mybir.dt.float8_e5m2_x4
+E4M3X4 = mybir.dt.float8_e4m3fn_x4
+ALU = mybir.AluOpType
+ACT = mybir.ActivationFunctionType
+
+P = 128
+D = 256
+K = 2 * D
+PACK = 4
+TOKENS = 8 * 8 * 128
+PER_PARTITION = TOKENS // P
+SLOTS = 4
+CHUNKS = PER_PARTITION // SLOTS
+SLOTS_PER_BANK = 2
+N_PASS = 512
+AHEAD = 2
+
+FLOPS = 2 * TOKENS * K * D
+BYTES = TOKENS * D * (2 + 4 + 4 + 2 + 4) + 2 * D * D * 2
+
+
+def by_partition(dram):
+    return dram.flatten_outer_dims().rearrange("(p n) d -> p n d", n=PER_PARTITION)
+
+
+def transpose_k_onto_partitions(nc, ident, bank, rows):
+    every_fourth = rows.rearrange("r (p t) -> r t p", t=PACK)
+    for t in range(PACK):
+        nc.tensor.transpose(bank[:, t, :], every_fourth[:, t, :], ident)
+
+
+def tile_scan_pb_t_v_kernel(
+    tc, query, wc, w_lin, b_lin, w_gate, b_gate, upd, gate, grad_out, out
+):
+    nc = tc.nc
+    query_v, upd_v, gate_v, grad_v, out_v = (
+        by_partition(x) for x in (query, upd, gate, grad_out, out)
+    )
+
+    with ExitStack() as stack:
+        const = stack.enter_context(tc.tile_pool(name="const", bufs=1))
+        inputs = stack.enter_context(tc.tile_pool(name="inputs", bufs=AHEAD + 1))
+        work = stack.enter_context(tc.tile_pool(name="work", bufs=2))
+        direct = stack.enter_context(tc.tile_pool(name="direct", bufs=4))
+        flipped = stack.enter_context(tc.psum_pool(name="flipped", bufs=4))
+        sums = stack.enter_context(tc.psum_pool(name="sums", bufs=SLOTS))
+        stack.enter_context(tc.manual_schedule())
+        chunk_tiles = {}
+
+        def load(c):
+            tokens = slice(c * SLOTS, (c + 1) * SLOTS)
+            gate_in = inputs.tile([P, SLOTS, D], F32)
+            grad_in = inputs.tile([P, SLOTS, D], BF16)
+            upd_in = inputs.tile([P, SLOTS, D], F32)
+            query_in = inputs.tile([P, SLOTS, D], BF16)
+            nc.sync.dma_start(out=gate_in[:], in_=gate_v[:, tokens, :])
+            nc.sync.dma_start(out=grad_in[:], in_=grad_v[:, tokens, :])
+            nc.sync.dma_start(out=upd_in[:], in_=upd_v[:, tokens, :])
+            nc.sync.dma_start(out=query_in[:], in_=query_v[:, tokens, :])
+            chunk_tiles[c] = {"gate": gate_in, "grad": grad_in, "upd": upd_in, "query": query_in}
+
+        def square_upd(c):
+            upd_sq = work.tile([P, SLOTS, D], F32)
+            nc.scalar.activation(out=upd_sq[:], in_=chunk_tiles[c]["upd"][:], func=ACT.Square)
+            chunk_tiles[c]["upd_sq"] = upd_sq
+
+        def gradients(c):
+            t = chunk_tiles[c]
+            a, g, h, q = t["gate"], t["grad"], t["upd"], t["query"]
+            ga = direct.tile([P, SLOTS, D], F32)
+            neg_gb = work.tile([P, SLOTS, D], F32)
+            dz = work.tile([P, SLOTS, K], BF16)
+            nc.vector.tensor_tensor(out=ga[:], in0=g[:], in1=a[:], op=ALU.mult)
+            nc.vector.scalar_tensor_tensor(
+                out=neg_gb[:], in0=a[:], scalar=1.0, in1=g[:], op0=ALU.subtract, op1=ALU.mult
+            )
+            nc.vector.tensor_tensor(out=h[:], in0=h[:], in1=q[:], op=ALU.subtract)
+            nc.vector.tensor_tensor(out=a[:], in0=neg_gb[:], in1=a[:], op=ALU.mult)
+            nc.vector.scalar_tensor_tensor(
+                out=dz[:, :, 0:D], in0=t["upd_sq"][:], scalar=1.0, in1=neg_gb[:],
+                op0=ALU.subtract, op1=ALU.mult,
+            )
+            nc.vector.tensor_tensor(out=dz[:, :, D:K], in0=h[:], in1=a[:], op=ALU.mult)
+            t["ga"] = ga
+            t["dz"] = dz
+
+        def flip(c):
+            t = chunk_tiles[c]
+            grouped = work.tile([P, SLOTS, P, PACK], BF16, align_bytes=64)
+            for first in range(0, SLOTS, SLOTS_PER_BANK):
+                bank = flipped.tile([P, SLOTS_PER_BANK, PACK, P], BF16)
+                for s in range(SLOTS_PER_BANK):
+                    transpose_k_onto_partitions(nc, ident[:], bank[:, s], t["dz"][:, first + s, :])
+                nc.scalar.copy(
+                    out=grouped[:, first : first + SLOTS_PER_BANK],
+                    in_=bank[:].rearrange("p s t r -> p s r t"),
+                )
+            t["grouped"] = grouped
+
+        def quantise_and_multiply(c):
+            t = chunk_tiles[c]
+            dz_codes = work.tile([P, SLOTS * P], U32, align_bytes=64)
+            dz_scales = work.tile([P, SLOTS * P], U8, align_bytes=64)
+            nc.vector.quantize_mx(
+                out=dz_codes[:].bitcast(E5M2X4),
+                scales=dz_scales[:],
+                in_=t["grouped"][:].rearrange("p s r t -> p (s r t)"),
+            )
+            for s in range(SLOTS):
+                tile_cols = slice(s * P, (s + 1) * P)
+                acc = sums.tile([P, N_PASS], F32)
+                nc.tensor.matmul_mx(
+                    out=acc[:],
+                    lhsT=dz_codes[:, tile_cols].bitcast(E5M2X4),
+                    lhsT_scale=dz_scales[:, tile_cols],
+                    rhs=w_codes[:].bitcast(E4M3X4),
+                    rhs_scale=w_scales[:],
+                    start=True,
+                    stop=True,
+                )
+                t["acc", s] = acc
+
+        def add_and_store(c):
+            t = chunk_tiles[c]
+            ga = t["ga"]
+            for s in range(SLOTS):
+                nc.vector.tensor_tensor(
+                    out=ga[:, s, :], in0=t["acc", s][:, 0:D], in1=ga[:, s, :], op=ALU.add
+                )
+            nc.sync.dma_start(out=out_v[:, c * SLOTS : (c + 1) * SLOTS, :], in_=ga[:])
+
+        def step(c):
+            if c + AHEAD < CHUNKS:
+                load(c + AHEAD)
+            if c + 1 < CHUNKS:
+                square_upd(c + 1)
+            if c < CHUNKS:
+                gradients(c)
+                flip(c)
+            if c >= 2:
+                add_and_store(c - 2)
+            if 1 <= c <= CHUNKS:
+                quantise_and_multiply(c - 1)
+
+        for c in range(AHEAD):
+            load(c)
+
+        w_rows = const.tile([P, D // P, K], BF16)
+        nc.scalar.dma_start(
+            out=w_rows[:, :, 0:D], in_=w_lin[0:D, :].rearrange("(h r) k -> r h k", r=P)
+        )
+        nc.scalar.dma_start(
+            out=w_rows[:, :, D:K], in_=w_gate[0:D, :].rearrange("(h r) k -> r h k", r=P)
+        )
+        ident = const.tile([P, P], BF16)
+        make_identity(nc, ident[:])
+        w_grouped = const.tile([P, N_PASS * PACK], BF16, align_bytes=64)
+        nc.vector.memset(w_grouped[:, D * PACK :].bitcast(I32), 0)
+        w_bank = flipped.tile([P, D // P, PACK, P], BF16, tag="bank")
+        for half in range(D // P):
+            transpose_k_onto_partitions(nc, ident[:], w_bank[:, half], w_rows[:, half, :])
+        nc.scalar.copy(
+            out=w_grouped[:, 0 : D * PACK].rearrange("p (h r t) -> p h r t", r=P, t=PACK),
+            in_=w_bank[:].rearrange("p h t r -> p h r t"),
+        )
+        w_codes = const.tile([P, N_PASS], U32, align_bytes=64)
+        w_scales = const.tile([P, N_PASS], U8, align_bytes=64)
+
+        square_upd(0)
+        step(0)
+        nc.vector.quantize_mx(
+            out=w_codes[:].bitcast(E4M3X4), scales=w_scales[:], in_=w_grouped[:]
+        )
+        for c in range(1, CHUNKS + 2):
+            step(c)

@@ -17,13 +17,17 @@ P = 128
 D = 256
 K = 2 * D
 PACK = 4
+PAIR = 2
 TOKENS = 8 * 8 * 128
 PER_PARTITION = TOKENS // P
 SLOTS = 4
 CHUNKS = PER_PARTITION // SLOTS
-SLOTS_PER_BANK = 2
+GROUP = 2
+GROUPS_PER_CHUNK = SLOTS // GROUP
+GROUPS = CHUNKS * GROUPS_PER_CHUNK
+COLS = GROUP * P
 N_PASS = 512
-AHEAD = 2
+AHEAD = 3
 
 FLOPS = 2 * TOKENS * K * D
 BYTES = TOKENS * D * (2 + 4 + 4 + 2 + 4) + 2 * D * D * 2
@@ -31,12 +35,6 @@ BYTES = TOKENS * D * (2 + 4 + 4 + 2 + 4) + 2 * D * D * 2
 
 def by_partition(dram):
     return dram.flatten_outer_dims().rearrange("(p n) d -> p n d", n=PER_PARTITION)
-
-
-def transpose_k_onto_partitions(nc, ident, bank, rows):
-    every_fourth = rows.rearrange("r (p t) -> r t p", t=PACK)
-    for t in range(PACK):
-        nc.tensor.transpose(bank[:, t, :], every_fourth[:, t, :], ident)
 
 
 def tile_scan_pb_t_v_kernel(
@@ -50,12 +48,14 @@ def tile_scan_pb_t_v_kernel(
     with ExitStack() as stack:
         const = stack.enter_context(tc.tile_pool(name="const", bufs=1))
         inputs = stack.enter_context(tc.tile_pool(name="inputs", bufs=AHEAD + 1))
-        work = stack.enter_context(tc.tile_pool(name="work", bufs=2))
+        factors = stack.enter_context(tc.tile_pool(name="factors", bufs=4))
+        packed = stack.enter_context(tc.tile_pool(name="packed", bufs=3))
         direct = stack.enter_context(tc.tile_pool(name="direct", bufs=4))
-        flipped = stack.enter_context(tc.psum_pool(name="flipped", bufs=4))
-        sums = stack.enter_context(tc.psum_pool(name="sums", bufs=SLOTS))
+        flipped = stack.enter_context(tc.psum_pool(name="flipped", bufs=2))
+        sums = stack.enter_context(tc.psum_pool(name="sums", bufs=GROUPS_PER_CHUNK))
         stack.enter_context(tc.manual_schedule())
         chunk_tiles = {}
+        group_tiles = {}
 
         def load(c):
             tokens = slice(c * SLOTS, (c + 1) * SLOTS)
@@ -63,92 +63,116 @@ def tile_scan_pb_t_v_kernel(
             grad_in = inputs.tile([P, SLOTS, D], BF16)
             upd_in = inputs.tile([P, SLOTS, D], F32)
             query_in = inputs.tile([P, SLOTS, D], BF16)
-            nc.sync.dma_start(out=gate_in[:], in_=gate_v[:, tokens, :])
             nc.sync.dma_start(out=grad_in[:], in_=grad_v[:, tokens, :])
-            nc.sync.dma_start(out=upd_in[:], in_=upd_v[:, tokens, :])
             nc.sync.dma_start(out=query_in[:], in_=query_v[:, tokens, :])
+            nc.sync.dma_start(out=upd_in[:], in_=upd_v[:, tokens, :])
+            nc.sync.dma_start(out=gate_in[:], in_=gate_v[:, tokens, :])
             chunk_tiles[c] = {"gate": gate_in, "grad": grad_in, "upd": upd_in, "query": query_in}
 
-        def square_upd(c):
-            upd_sq = work.tile([P, SLOTS, D], F32)
-            nc.scalar.activation(out=upd_sq[:], in_=chunk_tiles[c]["upd"][:], func=ACT.Square)
-            chunk_tiles[c]["upd_sq"] = upd_sq
-
-        def gradients(c):
-            t = chunk_tiles[c]
-            a, g, h, q = t["gate"], t["grad"], t["upd"], t["query"]
-            ga = direct.tile([P, SLOTS, D], F32)
-            neg_gb = work.tile([P, SLOTS, D], F32)
-            dz = work.tile([P, SLOTS, K], BF16)
-            nc.vector.tensor_tensor(out=ga[:], in0=g[:], in1=a[:], op=ALU.mult)
-            nc.vector.scalar_tensor_tensor(
-                out=neg_gb[:], in0=a[:], scalar=1.0, in1=g[:], op0=ALU.subtract, op1=ALU.mult
+        def flip_inputs(g):
+            c, part = divmod(g, GROUPS_PER_CHUNK)
+            mine = chunk_tiles[c]
+            pairs = flipped.tile([P, 2, COLS], F32)
+            upd_t = flipped.tile([P, PAIR, COLS], F32)
+            gate_t = flipped.tile([P, PAIR, COLS], F32)
+            for s in range(GROUP):
+                slot = part * GROUP + s
+                cols = slice(s * P, (s + 1) * P)
+                nc.tensor.transpose(pairs[:, 0, cols], mine["grad"][:, slot, :].bitcast(F32), ident[:])
+                nc.tensor.transpose(pairs[:, 1, cols], mine["query"][:, slot, :].bitcast(F32), ident[:])
+            for name, flat in (("upd", upd_t), ("gate", gate_t)):
+                for s in range(GROUP):
+                    slot = part * GROUP + s
+                    every_second = mine[name][:, slot, :].rearrange("r (w e) -> r e w", e=PAIR)
+                    for e in range(PAIR):
+                        nc.tensor.transpose(
+                            flat[:, e, s * P : (s + 1) * P], every_second[:, e, :], ident[:]
+                        )
+            upd_sq = factors.tile([P, COLS, PAIR], F32)
+            pairs_sb = factors.tile([P, 2, COLS], F32)
+            nc.scalar.activation(
+                out=upd_sq[:], in_=upd_t[:].rearrange("w e n -> w n e"), func=ACT.Square
             )
-            nc.vector.tensor_tensor(out=h[:], in0=h[:], in1=q[:], op=ALU.subtract)
-            nc.vector.tensor_tensor(out=a[:], in0=neg_gb[:], in1=a[:], op=ALU.mult)
+            nc.scalar.copy(out=pairs_sb[:], in_=pairs[:])
+            nc.scalar.activation(out=upd_sq[:], in_=upd_sq[:], func=ACT.Copy, bias=-1.0, scale=1.0)
+            group_tiles[g] = {
+                "upd": upd_t[:].rearrange("w e n -> w n e"),
+                "gate": gate_t[:].rearrange("w e n -> w n e"),
+                "grad": pairs_sb[:, 0, :].bitcast(BF16).rearrange("w (n e) -> w n e", e=PAIR),
+                "query": pairs_sb[:, 1, :].bitcast(BF16).rearrange("w (n e) -> w n e", e=PAIR),
+                "upd_sq_m1": upd_sq,
+            }
+
+        def products(g):
+            c, part = divmod(g, GROUPS_PER_CHUNK)
+            mine = group_tiles[g]
+            if part == 0:
+                grouped = packed.tile([P, SLOTS * P, PACK], BF16, align_bytes=64)
+                chunk_tiles[c]["grouped"] = grouped
+            grouped = chunk_tiles[c]["grouped"]
+            neg_gb = factors.tile([P, COLS, PAIR], F32)
+            diff = factors.tile([P, COLS, PAIR], F32)
+            neg_gab = factors.tile([P, COLS, PAIR], F32)
             nc.vector.scalar_tensor_tensor(
-                out=dz[:, :, 0:D], in0=t["upd_sq"][:], scalar=1.0, in1=neg_gb[:],
+                out=neg_gb[:], in0=mine["gate"], scalar=1.0, in1=mine["grad"],
                 op0=ALU.subtract, op1=ALU.mult,
             )
-            nc.vector.tensor_tensor(out=dz[:, :, D:K], in0=h[:], in1=a[:], op=ALU.mult)
-            t["ga"] = ga
-            t["dz"] = dz
+            nc.vector.tensor_tensor(out=diff[:], in0=mine["upd"], in1=mine["query"], op=ALU.subtract)
+            nc.vector.tensor_tensor(out=neg_gab[:], in0=mine["gate"], in1=neg_gb[:], op=ALU.mult)
+            cols = slice(part * COLS, (part + 1) * COLS)
+            nc.gpsimd.tensor_tensor(
+                out=grouped[:, cols, 0:PAIR], in0=mine["upd_sq_m1"][:], in1=neg_gb[:], op=ALU.mult
+            )
+            nc.gpsimd.tensor_tensor(
+                out=grouped[:, cols, PAIR:PACK], in0=diff[:], in1=neg_gab[:], op=ALU.mult
+            )
 
-        def flip(c):
-            t = chunk_tiles[c]
-            grouped = work.tile([P, SLOTS, P, PACK], BF16, align_bytes=64)
-            for first in range(0, SLOTS, SLOTS_PER_BANK):
-                bank = flipped.tile([P, SLOTS_PER_BANK, PACK, P], BF16)
-                for s in range(SLOTS_PER_BANK):
-                    transpose_k_onto_partitions(nc, ident[:], bank[:, s], t["dz"][:, first + s, :])
-                nc.scalar.copy(
-                    out=grouped[:, first : first + SLOTS_PER_BANK],
-                    in_=bank[:].rearrange("p s t r -> p s r t"),
-                )
-            t["grouped"] = grouped
+        def direct_term(c):
+            mine = chunk_tiles[c]
+            ga = direct.tile([P, SLOTS, D], F32)
+            nc.vector.tensor_tensor(out=ga[:], in0=mine["grad"][:], in1=mine["gate"][:], op=ALU.mult)
+            mine["ga"] = ga
 
         def quantise_and_multiply(c):
-            t = chunk_tiles[c]
-            dz_codes = work.tile([P, SLOTS * P], U32, align_bytes=64)
-            dz_scales = work.tile([P, SLOTS * P], U8, align_bytes=64)
+            mine = chunk_tiles[c]
+            dz_codes = packed.tile([P, SLOTS * P], U32, align_bytes=64)
+            dz_scales = packed.tile([P, SLOTS * P], U8, align_bytes=64)
             nc.vector.quantize_mx(
                 out=dz_codes[:].bitcast(E5M2X4),
                 scales=dz_scales[:],
-                in_=t["grouped"][:].rearrange("p s r t -> p (s r t)"),
+                in_=mine["grouped"][:].rearrange("w n t -> w (n t)"),
             )
-            for s in range(SLOTS):
-                tile_cols = slice(s * P, (s + 1) * P)
-                acc = sums.tile([P, N_PASS], F32)
-                nc.tensor.matmul_mx(
-                    out=acc[:],
-                    lhsT=dz_codes[:, tile_cols].bitcast(E5M2X4),
-                    lhsT_scale=dz_scales[:, tile_cols],
-                    rhs=w_codes[:].bitcast(E4M3X4),
-                    rhs_scale=w_scales[:],
-                    start=True,
-                    stop=True,
-                )
-                t["acc", s] = acc
+            for part in range(GROUPS_PER_CHUNK):
+                acc = sums.tile([P, GROUP, D], F32)
+                for s in range(GROUP):
+                    tokens = slice((part * GROUP + s) * P, (part * GROUP + s + 1) * P)
+                    w_cols = slice(D - s * D, D - s * D + N_PASS)
+                    nc.tensor.matmul_mx(
+                        out=acc[:].rearrange("r s o -> r (s o)"),
+                        lhsT=dz_codes[:, tokens].bitcast(E5M2X4),
+                        lhsT_scale=dz_scales[:, tokens],
+                        rhs=w_codes[:, w_cols].bitcast(E4M3X4),
+                        rhs_scale=w_scales[:, w_cols],
+                        start=(s == 0),
+                        stop=(s == GROUP - 1),
+                    )
+                mine["acc", part] = acc
 
         def add_and_store(c):
-            t = chunk_tiles[c]
-            ga = t["ga"]
-            for s in range(SLOTS):
+            mine = chunk_tiles[c]
+            ga = mine["ga"]
+            for part in range(GROUPS_PER_CHUNK):
+                slots = slice(part * GROUP, (part + 1) * GROUP)
                 nc.vector.tensor_tensor(
-                    out=ga[:, s, :], in0=t["acc", s][:, 0:D], in1=ga[:, s, :], op=ALU.add
+                    out=ga[:, slots, :], in0=mine["acc", part][:], in1=ga[:, slots, :], op=ALU.add
                 )
             nc.sync.dma_start(out=out_v[:, c * SLOTS : (c + 1) * SLOTS, :], in_=ga[:])
 
-        def step(c):
-            if c + AHEAD < CHUNKS:
-                load(c + AHEAD)
-            if c + 1 < CHUNKS:
-                square_upd(c + 1)
-            if c < CHUNKS:
-                gradients(c)
-                flip(c)
-            if c >= 2:
+        def finish(c):
+            if 2 <= c:
                 add_and_store(c - 2)
+            if c < CHUNKS:
+                direct_term(c)
             if 1 <= c <= CHUNKS:
                 quantise_and_multiply(c - 1)
 
@@ -162,24 +186,41 @@ def tile_scan_pb_t_v_kernel(
         nc.scalar.dma_start(
             out=w_rows[:, :, D:K], in_=w_gate[0:D, :].rearrange("(h r) k -> r h k", r=P)
         )
-        ident = const.tile([P, P], BF16)
+        ident = const.tile([P, P], F32)
         make_identity(nc, ident[:])
-        w_grouped = const.tile([P, N_PASS * PACK], BF16, align_bytes=64)
-        nc.vector.memset(w_grouped[:, D * PACK :].bitcast(I32), 0)
-        w_bank = flipped.tile([P, D // P, PACK, P], BF16, tag="bank")
-        for half in range(D // P):
-            transpose_k_onto_partitions(nc, ident[:], w_bank[:, half], w_rows[:, half, :])
+        w_codes = const.tile([P, D + N_PASS], U32, align_bytes=64)
+        w_scales = const.tile([P, D + N_PASS], U8, align_bytes=64)
+        nc.vector.memset(w_codes[:].bitcast(I32), 0)
+        nc.vector.memset(w_scales[:].bitcast(I32), 0)
+        w_bank = flipped.tile([P, 2, D], F32, tag="pairs")
+        for b in range(2):
+            for half in range(D // P):
+                nc.tensor.transpose(
+                    w_bank[:, b, half * P : (half + 1) * P],
+                    w_rows[:, half, b * D : (b + 1) * D].bitcast(F32),
+                    ident[:],
+                )
+        w_grouped = const.tile([P, D * PACK], BF16, align_bytes=64)
         nc.scalar.copy(
-            out=w_grouped[:, 0 : D * PACK].rearrange("p (h r t) -> p h r t", r=P, t=PACK),
-            in_=w_bank[:].rearrange("p h t r -> p h r t"),
+            out=w_grouped[:].bitcast(F32).rearrange("w (o b) -> w o b", b=2),
+            in_=w_bank[:].rearrange("w b o -> w o b"),
         )
-        w_codes = const.tile([P, N_PASS], U32, align_bytes=64)
-        w_scales = const.tile([P, N_PASS], U8, align_bytes=64)
-
-        square_upd(0)
-        step(0)
         nc.vector.quantize_mx(
-            out=w_codes[:].bitcast(E4M3X4), scales=w_scales[:], in_=w_grouped[:]
+            out=w_codes[:, D : 2 * D].bitcast(E4M3X4),
+            scales=w_scales[:, D : 2 * D],
+            in_=w_grouped[:],
         )
-        for c in range(1, CHUNKS + 2):
-            step(c)
+
+        flip_inputs(0)
+        flip_inputs(1)
+        for g in range(GROUPS):
+            c, part = divmod(g, GROUPS_PER_CHUNK)
+            if part == 0 and c + AHEAD < CHUNKS:
+                load(c + AHEAD)
+            products(g)
+            if g + 2 < GROUPS:
+                flip_inputs(g + 2)
+            if part == GROUPS_PER_CHUNK - 1:
+                finish(c)
+        finish(CHUNKS)
+        finish(CHUNKS + 1)

@@ -52,6 +52,7 @@ def tile_scan_pb_t_v_kernel(
         packed = stack.enter_context(tc.tile_pool(name="packed", bufs=3))
         direct = stack.enter_context(tc.tile_pool(name="direct", bufs=4))
         flipped = stack.enter_context(tc.psum_pool(name="flipped", bufs=2))
+        words = stack.enter_context(tc.psum_pool(name="words", bufs=1))
         sums = stack.enter_context(tc.psum_pool(name="sums", bufs=GROUPS_PER_CHUNK))
         stack.enter_context(tc.manual_schedule())
         chunk_tiles = {}
@@ -72,7 +73,7 @@ def tile_scan_pb_t_v_kernel(
         def flip_inputs(g):
             c, part = divmod(g, GROUPS_PER_CHUNK)
             mine = chunk_tiles[c]
-            pairs = flipped.tile([P, 2, COLS], F32)
+            pairs = words.tile([P, 2, COLS], F32)
             upd_t = flipped.tile([P, PAIR, COLS], F32)
             gate_t = flipped.tile([P, PAIR, COLS], F32)
             for s in range(GROUP):
@@ -100,6 +101,7 @@ def tile_scan_pb_t_v_kernel(
                 "gate": gate_t[:].rearrange("w e n -> w n e"),
                 "grad": pairs_sb[:, 0, :].bitcast(BF16).rearrange("w (n e) -> w n e", e=PAIR),
                 "query": pairs_sb[:, 1, :].bitcast(BF16).rearrange("w (n e) -> w n e", e=PAIR),
+                "grad_words": pairs_sb[:, 0, :],
                 "upd_sq_m1": upd_sq,
             }
 
@@ -127,10 +129,20 @@ def tile_scan_pb_t_v_kernel(
                 out=grouped[:, cols, PAIR:PACK], in0=diff[:], in1=neg_gab[:], op=ALU.mult
             )
 
+        def grad_into_psum(c):
+            grad_back = words.tile([P, SLOTS, P], F32)
+            for slot in range(SLOTS):
+                part, s = divmod(slot, GROUP)
+                flat = group_tiles[c * GROUPS_PER_CHUNK + part]["grad_words"]
+                nc.tensor.transpose(grad_back[:, slot, :], flat[:, s * P : (s + 1) * P], ident[:])
+            chunk_tiles[c]["grad_back"] = grad_back
+
         def direct_term(c):
             mine = chunk_tiles[c]
             ga = direct.tile([P, SLOTS, D], F32)
-            nc.vector.tensor_tensor(out=ga[:], in0=mine["grad"][:], in1=mine["gate"][:], op=ALU.mult)
+            nc.vector.tensor_tensor(
+                out=ga[:], in0=mine["grad_back"][:].bitcast(BF16), in1=mine["gate"][:], op=ALU.mult
+            )
             mine["ga"] = ga
 
         def quantise_and_multiply(c):
@@ -171,10 +183,10 @@ def tile_scan_pb_t_v_kernel(
         def finish(c):
             if 2 <= c:
                 add_and_store(c - 2)
-            if c < CHUNKS:
-                direct_term(c)
             if 1 <= c <= CHUNKS:
                 quantise_and_multiply(c - 1)
+            if c < CHUNKS:
+                direct_term(c)
 
         for c in range(AHEAD):
             load(c)
@@ -192,7 +204,7 @@ def tile_scan_pb_t_v_kernel(
         w_scales = const.tile([P, D + N_PASS], U8, align_bytes=64)
         nc.vector.memset(w_codes[:].bitcast(I32), 0)
         nc.vector.memset(w_scales[:].bitcast(I32), 0)
-        w_bank = flipped.tile([P, 2, D], F32, tag="pairs")
+        w_bank = words.tile([P, 2, D], F32, tag="pairs")
         for b in range(2):
             for half in range(D // P):
                 nc.tensor.transpose(
@@ -220,6 +232,8 @@ def tile_scan_pb_t_v_kernel(
             products(g)
             if g + 2 < GROUPS:
                 flip_inputs(g + 2)
+            if part == 0:
+                grad_into_psum(c)
             if part == GROUPS_PER_CHUNK - 1:
                 finish(c)
         finish(CHUNKS)

@@ -59,15 +59,17 @@ def tile_scan_pb_t_v_kernel(
         group_tiles = {}
 
         def load(c):
-            tokens = slice(c * SLOTS, (c + 1) * SLOTS)
             gate_in = inputs.tile([P, SLOTS, D], F32)
             grad_in = inputs.tile([P, SLOTS, D], BF16)
             upd_in = inputs.tile([P, SLOTS, D], F32)
             query_in = inputs.tile([P, SLOTS, D], BF16)
-            nc.sync.dma_start(out=grad_in[:], in_=grad_v[:, tokens, :])
-            nc.sync.dma_start(out=query_in[:], in_=query_v[:, tokens, :])
-            nc.sync.dma_start(out=upd_in[:], in_=upd_v[:, tokens, :])
-            nc.sync.dma_start(out=gate_in[:], in_=gate_v[:, tokens, :])
+            for part in range(GROUPS_PER_CHUNK):
+                slots = slice(part * GROUP, (part + 1) * GROUP)
+                tokens = slice(c * SLOTS + part * GROUP, c * SLOTS + (part + 1) * GROUP)
+                nc.sync.dma_start(out=grad_in[:, slots, :], in_=grad_v[:, tokens, :])
+                nc.sync.dma_start(out=query_in[:, slots, :], in_=query_v[:, tokens, :])
+                nc.sync.dma_start(out=gate_in[:, slots, :], in_=gate_v[:, tokens, :])
+                nc.sync.dma_start(out=upd_in[:, slots, :], in_=upd_v[:, tokens, :])
             chunk_tiles[c] = {"gate": gate_in, "grad": grad_in, "upd": upd_in, "query": query_in}
 
         def flip_inputs(g):
@@ -81,7 +83,7 @@ def tile_scan_pb_t_v_kernel(
                 cols = slice(s * P, (s + 1) * P)
                 nc.tensor.transpose(pairs[:, 0, cols], mine["grad"][:, slot, :].bitcast(F32), ident[:])
                 nc.tensor.transpose(pairs[:, 1, cols], mine["query"][:, slot, :].bitcast(F32), ident[:])
-            for name, flat in (("upd", upd_t), ("gate", gate_t)):
+            for name, flat in (("gate", gate_t), ("upd", upd_t)):
                 for s in range(GROUP):
                     slot = part * GROUP + s
                     every_second = mine[name][:, slot, :].rearrange("r (w e) -> r e w", e=PAIR)
@@ -91,10 +93,10 @@ def tile_scan_pb_t_v_kernel(
                         )
             upd_sq = factors.tile([P, COLS, PAIR], F32)
             pairs_sb = factors.tile([P, 2, COLS], F32)
+            nc.scalar.copy(out=pairs_sb[:], in_=pairs[:])
             nc.scalar.activation(
                 out=upd_sq[:], in_=upd_t[:].rearrange("w e n -> w n e"), func=ACT.Square
             )
-            nc.scalar.copy(out=pairs_sb[:], in_=pairs[:])
             nc.scalar.activation(out=upd_sq[:], in_=upd_sq[:], func=ACT.Copy, bias=-1.0, scale=1.0)
             group_tiles[g] = {
                 "upd": upd_t[:].rearrange("w e n -> w n e"),
@@ -175,10 +177,11 @@ def tile_scan_pb_t_v_kernel(
             ga = mine["ga"]
             for part in range(GROUPS_PER_CHUNK):
                 slots = slice(part * GROUP, (part + 1) * GROUP)
+                tokens = slice(c * SLOTS + part * GROUP, c * SLOTS + (part + 1) * GROUP)
                 nc.vector.tensor_tensor(
                     out=ga[:, slots, :], in0=mine["acc", part][:], in1=ga[:, slots, :], op=ALU.add
                 )
-            nc.sync.dma_start(out=out_v[:, c * SLOTS : (c + 1) * SLOTS, :], in_=ga[:])
+                nc.sync.dma_start(out=out_v[:, tokens, :], in_=ga[:, slots, :])
 
         def finish(c):
             if 2 <= c:
@@ -188,23 +191,38 @@ def tile_scan_pb_t_v_kernel(
             if c < CHUNKS:
                 direct_term(c)
 
-        for c in range(AHEAD):
-            load(c)
+        def step(g):
+            c, part = divmod(g, GROUPS_PER_CHUNK)
+            if part == 0 and c + AHEAD < CHUNKS:
+                load(c + AHEAD)
+            products(g)
+            if g + 2 < GROUPS:
+                flip_inputs(g + 2)
+            if part == 0:
+                grad_into_psum(c)
+            if part == GROUPS_PER_CHUNK - 1:
+                finish(c)
 
+        load(0)
         w_rows = const.tile([P, D // P, K], BF16)
-        nc.scalar.dma_start(
+        nc.sync.dma_start(
             out=w_rows[:, :, 0:D], in_=w_lin[0:D, :].rearrange("(h r) k -> r h k", r=P)
         )
-        nc.scalar.dma_start(
+        nc.sync.dma_start(
             out=w_rows[:, :, D:K], in_=w_gate[0:D, :].rearrange("(h r) k -> r h k", r=P)
         )
+        for c in range(1, AHEAD):
+            load(c)
         ident = const.tile([P, P], F32)
         make_identity(nc, ident[:])
         w_codes = const.tile([P, D + N_PASS], U32, align_bytes=64)
         w_scales = const.tile([P, D + N_PASS], U8, align_bytes=64)
         nc.vector.memset(w_codes[:].bitcast(I32), 0)
         nc.vector.memset(w_scales[:].bitcast(I32), 0)
-        w_bank = words.tile([P, 2, D], F32, tag="pairs")
+        flip_inputs(0)
+        flip_inputs(1)
+
+        w_bank = sums.tile([P, 2, D], F32, tag="acc")
         for b in range(2):
             for half in range(D // P):
                 nc.tensor.transpose(
@@ -217,24 +235,15 @@ def tile_scan_pb_t_v_kernel(
             out=w_grouped[:].bitcast(F32).rearrange("w (o b) -> w o b", b=2),
             in_=w_bank[:].rearrange("w b o -> w o b"),
         )
+        for g in range(GROUPS_PER_CHUNK):
+            step(g)
         nc.vector.quantize_mx(
             out=w_codes[:, D : 2 * D].bitcast(E4M3X4),
             scales=w_scales[:, D : 2 * D],
             in_=w_grouped[:],
         )
 
-        flip_inputs(0)
-        flip_inputs(1)
-        for g in range(GROUPS):
-            c, part = divmod(g, GROUPS_PER_CHUNK)
-            if part == 0 and c + AHEAD < CHUNKS:
-                load(c + AHEAD)
-            products(g)
-            if g + 2 < GROUPS:
-                flip_inputs(g + 2)
-            if part == 0:
-                grad_into_psum(c)
-            if part == GROUPS_PER_CHUNK - 1:
-                finish(c)
+        for g in range(GROUPS_PER_CHUNK, GROUPS):
+            step(g)
         finish(CHUNKS)
         finish(CHUNKS + 1)

@@ -107,20 +107,25 @@ def tile_scan_pb_t_v_kernel(
                 "upd_sq_m1": upd_sq,
             }
 
-        def products(g):
+        def first_factor(g):
+            mine = group_tiles[g]
+            neg_gb = factors.tile([P, COLS, PAIR], F32)
+            nc.vector.scalar_tensor_tensor(
+                out=neg_gb[:], in0=mine["gate"], scalar=1.0, in1=mine["grad"],
+                op0=ALU.subtract, op1=ALU.mult,
+            )
+            mine["neg_gb"] = neg_gb
+
+        def other_products(g):
             c, part = divmod(g, GROUPS_PER_CHUNK)
             mine = group_tiles[g]
             if part == 0:
                 grouped = packed.tile([P, SLOTS * P, PACK], BF16, align_bytes=64)
                 chunk_tiles[c]["grouped"] = grouped
             grouped = chunk_tiles[c]["grouped"]
-            neg_gb = factors.tile([P, COLS, PAIR], F32)
+            neg_gb = mine["neg_gb"]
             diff = factors.tile([P, COLS, PAIR], F32)
             neg_gab = factors.tile([P, COLS, PAIR], F32)
-            nc.vector.scalar_tensor_tensor(
-                out=neg_gb[:], in0=mine["gate"], scalar=1.0, in1=mine["grad"],
-                op0=ALU.subtract, op1=ALU.mult,
-            )
             nc.vector.tensor_tensor(out=diff[:], in0=mine["upd"], in1=mine["query"], op=ALU.subtract)
             nc.vector.tensor_tensor(out=neg_gab[:], in0=mine["gate"], in1=neg_gb[:], op=ALU.mult)
             cols = slice(part * COLS, (part + 1) * COLS)
@@ -183,25 +188,22 @@ def tile_scan_pb_t_v_kernel(
                 )
                 nc.sync.dma_start(out=out_v[:, tokens, :], in_=ga[:, slots, :])
 
-        def finish(c):
-            if 2 <= c:
-                add_and_store(c - 2)
-            if 1 <= c <= CHUNKS:
-                quantise_and_multiply(c - 1)
-            if c < CHUNKS:
-                direct_term(c)
-
         def step(g):
             c, part = divmod(g, GROUPS_PER_CHUNK)
-            if part == 0 and c + AHEAD < CHUNKS:
-                load(c + AHEAD)
-            products(g)
+            if part == 0:
+                if c + AHEAD < CHUNKS:
+                    load(c + AHEAD)
+                grad_into_psum(c)
+            first_factor(g)
+            if part == 0 and c >= 1:
+                quantise_and_multiply(c - 1)
+            other_products(g)
             if g + 2 < GROUPS:
                 flip_inputs(g + 2)
-            if part == 0:
-                grad_into_psum(c)
             if part == GROUPS_PER_CHUNK - 1:
-                finish(c)
+                direct_term(c)
+                if c >= 1:
+                    add_and_store(c - 1)
 
         load(0)
         w_rows = const.tile([P, D // P, K], BF16)
@@ -245,5 +247,5 @@ def tile_scan_pb_t_v_kernel(
 
         for g in range(GROUPS_PER_CHUNK, GROUPS):
             step(g)
-        finish(CHUNKS)
-        finish(CHUNKS + 1)
+        quantise_and_multiply(CHUNKS - 1)
+        add_and_store(CHUNKS - 1)

@@ -47,12 +47,14 @@ def tile_scan_pb_t_v_kernel(
 
     with ExitStack() as stack:
         const = stack.enter_context(tc.tile_pool(name="const", bufs=1))
-        inputs = stack.enter_context(tc.tile_pool(name="inputs", bufs=AHEAD + 1))
-        factors = stack.enter_context(tc.tile_pool(name="factors", bufs=4))
+        inputs = stack.enter_context(tc.tile_pool(name="inputs", bufs=AHEAD + 2))
+        prepared = stack.enter_context(tc.tile_pool(name="prepared", bufs=4))
+        factors = stack.enter_context(tc.tile_pool(name="factors", bufs=3))
         packed = stack.enter_context(tc.tile_pool(name="packed", bufs=3))
-        direct = stack.enter_context(tc.tile_pool(name="direct", bufs=4))
-        flipped = stack.enter_context(tc.psum_pool(name="flipped", bufs=2))
-        words = stack.enter_context(tc.psum_pool(name="words", bufs=1))
+        direct = stack.enter_context(tc.tile_pool(name="direct", bufs=8))
+        gate_banks = stack.enter_context(tc.psum_pool(name="gate_banks", bufs=2))
+        grad_banks = stack.enter_context(tc.psum_pool(name="grad_banks", bufs=1))
+        right_banks = stack.enter_context(tc.psum_pool(name="right_banks", bufs=3))
         sums = stack.enter_context(tc.psum_pool(name="sums", bufs=GROUPS_PER_CHUNK))
         stack.enter_context(tc.manual_schedule())
         chunk_tiles = {}
@@ -67,92 +69,130 @@ def tile_scan_pb_t_v_kernel(
                 slots = slice(part * GROUP, (part + 1) * GROUP)
                 tokens = slice(c * SLOTS + part * GROUP, c * SLOTS + (part + 1) * GROUP)
                 nc.sync.dma_start(out=grad_in[:, slots, :], in_=grad_v[:, tokens, :])
-                nc.sync.dma_start(out=query_in[:, slots, :], in_=query_v[:, tokens, :])
                 nc.sync.dma_start(out=gate_in[:, slots, :], in_=gate_v[:, tokens, :])
                 nc.sync.dma_start(out=upd_in[:, slots, :], in_=upd_v[:, tokens, :])
-            chunk_tiles[c] = {"gate": gate_in, "grad": grad_in, "upd": upd_in, "query": query_in}
+                nc.sync.dma_start(out=query_in[:, slots, :], in_=query_v[:, tokens, :])
+                group_tiles[c * GROUPS_PER_CHUNK + part] = {
+                    "gate_in": gate_in[:, slots, :],
+                    "grad_in": grad_in[:, slots, :],
+                    "upd_in": upd_in[:, slots, :],
+                    "query_in": query_in[:, slots, :],
+                }
+            chunk_tiles[c] = {}
 
-        def flip_inputs(g):
-            c, part = divmod(g, GROUPS_PER_CHUNK)
-            mine = chunk_tiles[c]
-            pairs = words.tile([P, 2, COLS], F32)
-            upd_t = flipped.tile([P, PAIR, COLS], F32)
-            gate_t = flipped.tile([P, PAIR, COLS], F32)
-            for s in range(GROUP):
-                slot = part * GROUP + s
-                cols = slice(s * P, (s + 1) * P)
-                nc.tensor.transpose(pairs[:, 0, cols], mine["grad"][:, slot, :].bitcast(F32), ident[:])
-                nc.tensor.transpose(pairs[:, 1, cols], mine["query"][:, slot, :].bitcast(F32), ident[:])
-            for name, flat in (("gate", gate_t), ("upd", upd_t)):
-                for s in range(GROUP):
-                    slot = part * GROUP + s
-                    every_second = mine[name][:, slot, :].rearrange("r (w e) -> r e w", e=PAIR)
-                    for e in range(PAIR):
-                        nc.tensor.transpose(
-                            flat[:, e, s * P : (s + 1) * P], every_second[:, e, :], ident[:]
-                        )
-            upd_sq = factors.tile([P, COLS, PAIR], F32)
-            pairs_sb = factors.tile([P, 2, COLS], F32)
-            nc.scalar.copy(out=pairs_sb[:], in_=pairs[:])
-            nc.scalar.activation(
-                out=upd_sq[:], in_=upd_t[:].rearrange("w e n -> w n e"), func=ACT.Square
-            )
-            nc.scalar.activation(out=upd_sq[:], in_=upd_sq[:], func=ACT.Copy, bias=-1.0, scale=1.0)
-            group_tiles[g] = {
-                "upd": upd_t[:].rearrange("w e n -> w n e"),
-                "gate": gate_t[:].rearrange("w e n -> w n e"),
-                "grad": pairs_sb[:, 0, :].bitcast(BF16).rearrange("w (n e) -> w n e", e=PAIR),
-                "query": pairs_sb[:, 1, :].bitcast(BF16).rearrange("w (n e) -> w n e", e=PAIR),
-                "grad_words": pairs_sb[:, 0, :],
-                "upd_sq_m1": upd_sq,
-            }
-
-        def first_factor(g):
+        def square_and_negate(g):
             mine = group_tiles[g]
-            neg_gb = factors.tile([P, COLS, PAIR], F32)
-            nc.vector.scalar_tensor_tensor(
-                out=neg_gb[:], in0=mine["gate"], scalar=1.0, in1=mine["grad"],
-                op0=ALU.subtract, op1=ALU.mult,
+            upd_sq = prepared.tile([P, GROUP, PAIR, P], F32)
+            neg_query = prepared.tile([P, GROUP, PAIR, P], F32)
+            nc.scalar.activation(
+                out=upd_sq[:],
+                in_=mine["upd_in"].rearrange("r s (w e) -> r s e w", e=PAIR),
+                func=ACT.Square,
             )
-            mine["neg_gb"] = neg_gb
+            nc.scalar.activation(
+                out=neg_query[:],
+                in_=mine["query_in"].rearrange("r s (w e) -> r s e w", e=PAIR),
+                func=ACT.Copy,
+                scale=-1.0,
+            )
+            mine["upd_sq"] = upd_sq
+            mine["neg_query"] = neg_query
 
-        def other_products(g):
+        def subtract_one(g):
+            upd_sq = group_tiles[g]["upd_sq"]
+            nc.scalar.activation(out=upd_sq[:], in_=upd_sq[:], func=ACT.Copy, bias=-1.0, scale=1.0)
+
+        def flip_gate(g):
             c, part = divmod(g, GROUPS_PER_CHUNK)
             mine = group_tiles[g]
             if part == 0:
-                grouped = packed.tile([P, SLOTS * P, PACK], BF16, align_bytes=64)
-                chunk_tiles[c]["grouped"] = grouped
-            grouped = chunk_tiles[c]["grouped"]
-            neg_gb = mine["neg_gb"]
-            diff = factors.tile([P, COLS, PAIR], F32)
-            neg_gab = factors.tile([P, COLS, PAIR], F32)
-            nc.vector.tensor_tensor(out=diff[:], in0=mine["upd"], in1=mine["query"], op=ALU.subtract)
-            nc.vector.tensor_tensor(out=neg_gab[:], in0=mine["gate"], in1=neg_gb[:], op=ALU.mult)
-            cols = slice(part * COLS, (part + 1) * COLS)
-            nc.gpsimd.tensor_tensor(
-                out=grouped[:, cols, 0:PAIR], in0=mine["upd_sq_m1"][:], in1=neg_gb[:], op=ALU.mult
+                grad_words = grad_banks.tile([P, SLOTS * P], F32)
+                for slot in range(SLOTS):
+                    h, s = divmod(slot, GROUP)
+                    nc.tensor.transpose(
+                        grad_words[:, slot * P : (slot + 1) * P],
+                        group_tiles[g + h]["grad_in"][:, s, :].bitcast(F32),
+                        ident[:],
+                    )
+                chunk_tiles[c]["grad_words"] = grad_words
+            gate_t = gate_banks.tile([P, PAIR, COLS], F32)
+            for s in range(GROUP):
+                every_second = mine["gate_in"][:, s, :].rearrange("r (w e) -> r e w", e=PAIR)
+                for e in range(PAIR):
+                    nc.tensor.transpose(
+                        gate_t[:, e, s * P : (s + 1) * P], every_second[:, e, :], ident[:]
+                    )
+            mine["gate_t"] = gate_t[:].rearrange("w e n -> w n e")
+
+        def copy_gate(g):
+            c, part = divmod(g, GROUPS_PER_CHUNK)
+            mine = group_tiles[g]
+            if part == 0:
+                grad_sb = factors.tile([P, SLOTS * P], F32)
+                nc.scalar.copy(out=grad_sb[:], in_=chunk_tiles[c]["grad_words"][:])
+                chunk_tiles[c]["grad_sb"] = grad_sb
+            gate_sb = factors.tile([P, COLS, PAIR], F32)
+            nc.scalar.copy(out=gate_sb[:], in_=mine["gate_t"])
+            mine["gate_sb"] = gate_sb
+            grad_pairs = chunk_tiles[c]["grad_sb"][:, part * COLS : (part + 1) * COLS]
+            mine["grad_t"] = grad_pairs.bitcast(BF16).rearrange("w (n e) -> w n e", e=PAIR)
+
+        def flip_right(g, s):
+            mine = group_tiles[g]
+            right = right_banks.tile([P, 2, PAIR, P], F32)
+            upd_pairs = mine["upd_in"][:, s, :].rearrange("r (w e) -> r e w", e=PAIR)
+            for e in range(PAIR):
+                nc.tensor.transpose(right[:, 0, e, :], mine["upd_sq"][:, s, e, :], ident[:])
+            for e in range(PAIR):
+                nc.tensor.matmul(
+                    out=right[:, 1, e, :], lhsT=upd_pairs[:, e, :], rhs=ident[:],
+                    start=True, stop=False, is_transpose=True,
+                )
+                nc.tensor.matmul(
+                    out=right[:, 1, e, :], lhsT=mine["neg_query"][:, s, e, :], rhs=ident[:],
+                    start=False, stop=True, is_transpose=True,
+                )
+            mine["right", s] = right
+
+        def first_left(g):
+            mine = group_tiles[g]
+            left = factors.tile([P, 2, COLS, PAIR], F32)
+            nc.vector.scalar_tensor_tensor(
+                out=left[:, 0, :, :], in0=mine["gate_t"], scalar=1.0, in1=mine["grad_t"],
+                op0=ALU.subtract, op1=ALU.mult,
             )
+            mine["left"] = left
+
+        def second_left(g):
+            mine = group_tiles[g]
+            left = mine["left"]
             nc.gpsimd.tensor_tensor(
-                out=grouped[:, cols, PAIR:PACK], in0=diff[:], in1=neg_gab[:], op=ALU.mult
+                out=left[:, 1, :, :], in0=mine["gate_sb"][:], in1=left[:, 0, :, :], op=ALU.mult
             )
 
-        def grad_into_psum(c):
-            grad_back = words.tile([P, SLOTS, P], F32)
-            for slot in range(SLOTS):
-                part, s = divmod(slot, GROUP)
-                flat = group_tiles[c * GROUPS_PER_CHUNK + part]["grad_words"]
-                nc.tensor.transpose(grad_back[:, slot, :], flat[:, s * P : (s + 1) * P], ident[:])
-            chunk_tiles[c]["grad_back"] = grad_back
-
-        def direct_term(c):
-            mine = chunk_tiles[c]
-            ga = direct.tile([P, SLOTS, D], F32)
-            nc.vector.tensor_tensor(
-                out=ga[:], in0=mine["grad_back"][:].bitcast(BF16), in1=mine["gate"][:], op=ALU.mult
-            )
+        def direct_term(g):
+            mine = group_tiles[g]
+            ga = direct.tile([P, GROUP, D], F32)
+            nc.gpsimd.tensor_tensor(out=ga[:], in0=mine["grad_in"], in1=mine["gate_in"], op=ALU.mult)
             mine["ga"] = ga
 
-        def quantise_and_multiply(c):
+        def products(g, s):
+            c, part = divmod(g, GROUPS_PER_CHUNK)
+            mine = group_tiles[g]
+            if part == 0 and s == 0:
+                grouped = packed.tile([P, SLOTS * P, PACK], BF16, align_bytes=64)
+                chunk_tiles[c]["grouped"] = grouped
+            slot = part * GROUP + s
+            nc.vector.tensor_tensor(
+                out=chunk_tiles[c]["grouped"][:, slot * P : (slot + 1) * P, :].rearrange(
+                    "w n (b e) -> w n b e", e=PAIR
+                ),
+                in0=mine["right", s][:].rearrange("w b e n -> w n b e"),
+                in1=mine["left"][:, :, s * P : (s + 1) * P, :].rearrange("w b n e -> w n b e"),
+                op=ALU.mult,
+            )
+
+        def quantise(c):
             mine = chunk_tiles[c]
             dz_codes = packed.tile([P, SLOTS * P], U32, align_bytes=64)
             dz_scales = packed.tile([P, SLOTS * P], U8, align_bytes=64)
@@ -161,6 +201,11 @@ def tile_scan_pb_t_v_kernel(
                 scales=dz_scales[:],
                 in_=mine["grouped"][:].rearrange("w n t -> w (n t)"),
             )
+            mine["codes"] = dz_codes
+            mine["scales"] = dz_scales
+
+        def multiply(c):
+            mine = chunk_tiles[c]
             for part in range(GROUPS_PER_CHUNK):
                 acc = sums.tile([P, GROUP, D], F32)
                 for s in range(GROUP):
@@ -168,42 +213,49 @@ def tile_scan_pb_t_v_kernel(
                     w_cols = slice(D - s * D, D - s * D + N_PASS)
                     nc.tensor.matmul_mx(
                         out=acc[:].rearrange("r s o -> r (s o)"),
-                        lhsT=dz_codes[:, tokens].bitcast(E5M2X4),
-                        lhsT_scale=dz_scales[:, tokens],
+                        lhsT=mine["codes"][:, tokens].bitcast(E5M2X4),
+                        lhsT_scale=mine["scales"][:, tokens],
                         rhs=w_codes[:, w_cols].bitcast(E4M3X4),
                         rhs_scale=w_scales[:, w_cols],
                         start=(s == 0),
                         stop=(s == GROUP - 1),
                     )
-                mine["acc", part] = acc
+                group_tiles[c * GROUPS_PER_CHUNK + part]["acc"] = acc
 
-        def add_and_store(c):
-            mine = chunk_tiles[c]
-            ga = mine["ga"]
-            for part in range(GROUPS_PER_CHUNK):
-                slots = slice(part * GROUP, (part + 1) * GROUP)
-                tokens = slice(c * SLOTS + part * GROUP, c * SLOTS + (part + 1) * GROUP)
-                nc.vector.tensor_tensor(
-                    out=ga[:, slots, :], in0=mine["acc", part][:], in1=ga[:, slots, :], op=ALU.add
-                )
-                nc.sync.dma_start(out=out_v[:, tokens, :], in_=ga[:, slots, :])
+        def add_and_store(g):
+            ga = group_tiles[g]["ga"]
+            nc.vector.tensor_tensor(out=ga[:], in0=group_tiles[g]["acc"][:], in1=ga[:], op=ALU.add)
+            nc.sync.dma_start(out=out_v[:, g * GROUP : (g + 1) * GROUP, :], in_=ga[:])
 
-        def step(g):
-            c, part = divmod(g, GROUPS_PER_CHUNK)
-            if part == 0:
-                if c + AHEAD < CHUNKS:
-                    load(c + AHEAD)
-                grad_into_psum(c)
-            first_factor(g)
-            if part == 0 and c >= 1:
-                quantise_and_multiply(c - 1)
-            other_products(g)
-            if g + 2 < GROUPS:
-                flip_inputs(g + 2)
-            if part == GROUPS_PER_CHUNK - 1:
-                direct_term(c)
-                if c >= 1:
-                    add_and_store(c - 1)
+        def step(k):
+            c, part = divmod(k, GROUPS_PER_CHUNK)
+            if part == 0 and c + AHEAD < CHUNKS:
+                load(c + AHEAD)
+            if k + 1 < GROUPS:
+                flip_gate(k + 1)
+            if k < GROUPS:
+                flip_right(k, 0)
+                flip_right(k, 1)
+            if k + 2 < GROUPS:
+                square_and_negate(k + 2)
+            if k + 1 < GROUPS:
+                copy_gate(k + 1)
+            if k + 2 < GROUPS:
+                subtract_one(k + 2)
+            if 0 <= k - 4 < GROUPS:
+                add_and_store(k - 4)
+            if k < GROUPS:
+                first_left(k)
+            if part == 1 and 1 <= c <= CHUNKS:
+                quantise(c - 1)
+            if k < GROUPS:
+                second_left(k)
+                direct_term(k)
+            if 0 <= k - 1 < GROUPS:
+                products(k - 1, 0)
+                products(k - 1, 1)
+            if part == 1 and 1 <= c <= CHUNKS:
+                multiply(c - 1)
 
         load(0)
         w_rows = const.tile([P, D // P, K], BF16)
@@ -221,8 +273,13 @@ def tile_scan_pb_t_v_kernel(
         w_scales = const.tile([P, D + N_PASS], U8, align_bytes=64)
         nc.vector.memset(w_codes[:].bitcast(I32), 0)
         nc.vector.memset(w_scales[:].bitcast(I32), 0)
-        flip_inputs(0)
-        flip_inputs(1)
+        flip_gate(0)
+        copy_gate(0)
+        square_and_negate(0)
+        subtract_one(0)
+        square_and_negate(1)
+        subtract_one(1)
+        step(0)
 
         w_bank = sums.tile([P, 2, D], F32, tag="acc")
         for b in range(2):
@@ -237,15 +294,12 @@ def tile_scan_pb_t_v_kernel(
             out=w_grouped[:].bitcast(F32).rearrange("w (o b) -> w o b", b=2),
             in_=w_bank[:].rearrange("w b o -> w o b"),
         )
-        for g in range(GROUPS_PER_CHUNK):
-            step(g)
+        step(1)
         nc.vector.quantize_mx(
             out=w_codes[:, D : 2 * D].bitcast(E4M3X4),
             scales=w_scales[:, D : 2 * D],
             in_=w_grouped[:],
         )
 
-        for g in range(GROUPS_PER_CHUNK, GROUPS):
-            step(g)
-        quantise_and_multiply(CHUNKS - 1)
-        add_and_store(CHUNKS - 1)
+        for k in range(2, GROUPS + 4):
+            step(k)

@@ -24,11 +24,20 @@ SLOTS = 4
 CHUNKS = PER_PARTITION // SLOTS
 GROUP = 2
 GROUPS_PER_CHUNK = SLOTS // GROUP
-GROUPS = CHUNKS * GROUPS_PER_CHUNK
 COLS = GROUP * P
 N_PASS = 512
 AHEAD = 3
-
+ZERO = 0
+TBUFS = 3
+YSET = (1, 3)
+AD = 1
+ADMIN = 3
+PYMIN = 3
+ZC = (1, 2)
+TSMALL = 2
+G0 = 0
+MSPLIT = 2
+FIRST = 0
 FLOPS = 2 * TOKENS * K * D
 BYTES = TOKENS * D * (2 + 4 + 4 + 2 + 4) + 2 * D * D * 2
 
@@ -47,259 +56,311 @@ def tile_scan_pb_t_v_kernel(
 
     with ExitStack() as stack:
         const = stack.enter_context(tc.tile_pool(name="const", bufs=1))
-        inputs = stack.enter_context(tc.tile_pool(name="inputs", bufs=AHEAD + 2))
+        inputs = stack.enter_context(tc.tile_pool(name="inputs", bufs=6))
         prepared = stack.enter_context(tc.tile_pool(name="prepared", bufs=4))
         factors = stack.enter_context(tc.tile_pool(name="factors", bufs=3))
         packed = stack.enter_context(tc.tile_pool(name="packed", bufs=3))
-        direct = stack.enter_context(tc.tile_pool(name="direct", bufs=8))
+        direct = stack.enter_context(tc.tile_pool(name="direct", bufs=TBUFS))
         gate_banks = stack.enter_context(tc.psum_pool(name="gate_banks", bufs=2))
         grad_banks = stack.enter_context(tc.psum_pool(name="grad_banks", bufs=1))
         right_banks = stack.enter_context(tc.psum_pool(name="right_banks", bufs=3))
-        sums = stack.enter_context(tc.psum_pool(name="sums", bufs=GROUPS_PER_CHUNK))
+        sums = stack.enter_context(tc.psum_pool(name="sums", bufs=2))
         stack.enter_context(tc.manual_schedule())
-        chunk_tiles = {}
-        group_tiles = {}
+        diffs = stack.enter_context(tc.tile_pool(name="diffs", bufs=2))
+        results = stack.enter_context(tc.tile_pool(name="results", bufs=4))
+        chunk = {}
 
         def load(c):
             gate_in = inputs.tile([P, SLOTS, D], F32)
             grad_in = inputs.tile([P, SLOTS, D], BF16)
             upd_in = inputs.tile([P, SLOTS, D], F32)
             query_in = inputs.tile([P, SLOTS, D], BF16)
-            for part in range(GROUPS_PER_CHUNK):
-                slots = slice(part * GROUP, (part + 1) * GROUP)
-                tokens = slice(c * SLOTS + part * GROUP, c * SLOTS + (part + 1) * GROUP)
-                nc.sync.dma_start(out=grad_in[:, slots, :], in_=grad_v[:, tokens, :])
-                nc.sync.dma_start(out=gate_in[:, slots, :], in_=gate_v[:, tokens, :])
-                nc.sync.dma_start(out=upd_in[:, slots, :], in_=upd_v[:, tokens, :])
-                nc.sync.dma_start(out=query_in[:, slots, :], in_=query_v[:, tokens, :])
-                group_tiles[c * GROUPS_PER_CHUNK + part] = {
-                    "gate_in": gate_in[:, slots, :],
-                    "grad_in": grad_in[:, slots, :],
-                    "upd_in": upd_in[:, slots, :],
-                    "query_in": query_in[:, slots, :],
-                }
-            chunk_tiles[c] = {}
+            parts = ((0, 2), (2, 4)) if c < 1 else ((0, 4),)
+            for lo, hi in parts:
+                for t, v in ((grad_in, grad_v), (gate_in, gate_v), (upd_in, upd_v), (query_in, query_v)):
+                    nc.sync.dma_start(out=t[:, lo:hi, :], in_=v[:, c * SLOTS + lo : c * SLOTS + hi, :])
+            chunk[c] = {"gate": gate_in, "grad": grad_in, "upd": upd_in, "query": query_in}
 
-        def square_and_negate(g):
-            mine = group_tiles[g]
-            upd_sq = prepared.tile([P, GROUP, PAIR, P], F32)
-            neg_query = prepared.tile([P, GROUP, PAIR, P], F32)
-            nc.scalar.activation(
-                out=upd_sq[:],
-                in_=mine["upd_in"].rearrange("r s (w e) -> r s e w", e=PAIR),
-                func=ACT.Square,
-            )
-            nc.scalar.activation(
-                out=neg_query[:],
-                in_=mine["query_in"].rearrange("r s (w e) -> r s e w", e=PAIR),
-                func=ACT.Copy,
-                scale=-1.0,
-            )
-            mine["upd_sq"] = upd_sq
-            mine["neg_query"] = neg_query
+        def pieces(c):
+            return ((0, 2), (2, 4)) if c < 1 else ((0, 4),)
 
-        def subtract_one(g):
-            upd_sq = group_tiles[g]["upd_sq"]
-            nc.scalar.activation(out=upd_sq[:], in_=upd_sq[:], func=ACT.Copy, bias=-1.0, scale=1.0)
+        def de(ap):
+            return ap.rearrange("r s (w e) -> r s e w", e=PAIR)
 
-        def flip_gate(g):
-            c, part = divmod(g, GROUPS_PER_CHUNK)
-            mine = group_tiles[g]
-            if part == 0:
-                grad_words = grad_banks.tile([P, SLOTS * P], F32)
-                for slot in range(SLOTS):
-                    h, s = divmod(slot, GROUP)
-                    nc.tensor.transpose(
-                        grad_words[:, slot * P : (slot + 1) * P],
-                        group_tiles[g + h]["grad_in"][:, s, :].bitcast(F32),
-                        ident[:],
-                    )
-                chunk_tiles[c]["grad_words"] = grad_words
+        def by_py(c, h):
+            return (2 * c + h) % 4 in YSET and c >= PYMIN
+
+        def prep(c, what, lo, hi):
+            m = chunk[c]
+            sl = slice(lo, hi)
+            if what == "sq":
+                if lo == 0:
+                    upd_sq = prepared.tile([P, SLOTS, PAIR, P], F32)
+                    m["upd_sq"] = upd_sq
+                nc.scalar.activation(out=m["upd_sq"][:, sl], in_=de(m["upd"][:, sl, :]), func=ACT.Square)
+            elif what == "ng":
+                if any(by_py(c, h) for h in range(2)):
+                    neg_grad = prepared.tile([P, SLOTS, PAIR, P], F32)
+                    m["neg_grad"] = neg_grad
+                    for h in range(2):
+                        if by_py(c, h):
+                            nc.scalar.activation(out=neg_grad[:, 2 * h : 2 * h + 2], in_=de(m["grad"][:, 2 * h : 2 * h + 2, :]), func=ACT.Copy, scale=-1.0)
+            elif what == "nq":
+                neg_query = prepared.tile([P, SLOTS, PAIR, P], F32)
+                m["neg_query"] = neg_query
+                nc.scalar.activation(out=neg_query[:], in_=de(m["query"][:]), func=ACT.Copy, scale=-1.0)
+            elif what == "ad":
+                if lo == 0:
+                    gate_de = prepared.tile([P, SLOTS, PAIR, P], F32)
+                    m["gate_de"] = gate_de
+                nc.scalar.copy(out=m["gate_de"][:, sl], in_=de(m["gate"][:, sl, :]))
+            else:
+                nc.scalar.activation(out=m["upd_sq"][:, sl], in_=m["upd_sq"][:, sl], func=ACT.Copy, bias=-1.0, scale=1.0)
+
+        def flip_grad(c, h):
+            m = chunk[c]
+            if by_py(c, h):
+                neg_gb = grad_banks.tile([P, PAIR, COLS], F32, tag="grad_words")
+                for s in range(GROUP):
+                    for e in range(PAIR):
+                        o = neg_gb[:, e, s * P : (s + 1) * P]
+                        nc.tensor.matmul(out=o, lhsT=m["ga"][:, h * GROUP + s, e, :], rhs=ident[:], start=True, stop=False, is_transpose=True)
+                        nc.tensor.matmul(out=o, lhsT=m["neg_grad"][:, h * GROUP + s, e, :], rhs=ident[:], start=False, stop=True, is_transpose=True)
+                m["neg_gb", h] = neg_gb
+            else:
+                grad_words = grad_banks.tile([P, COLS], F32)
+                for s in range(GROUP):
+                    nc.tensor.transpose(grad_words[:, s * P : (s + 1) * P], m["grad"][:, h * GROUP + s, :].bitcast(F32), ident[:])
+                m["grad_words", h] = grad_words
+
+        def flip_gate(c, h):
+            m = chunk[c]
             gate_t = gate_banks.tile([P, PAIR, COLS], F32)
             for s in range(GROUP):
-                every_second = mine["gate_in"][:, s, :].rearrange("r (w e) -> r e w", e=PAIR)
                 for e in range(PAIR):
-                    nc.tensor.transpose(
-                        gate_t[:, e, s * P : (s + 1) * P], every_second[:, e, :], ident[:]
-                    )
-            mine["gate_t"] = gate_t[:].rearrange("w e n -> w n e")
+                    if AD and c >= ADMIN:
+                        src = m["gate_de"][:, h * GROUP + s, e, :]
+                    else:
+                        src = m["gate"][:, h * GROUP + s, :].rearrange("r (w e) -> r e w", e=PAIR)[:, e, :]
+                    nc.tensor.transpose(gate_t[:, e, s * P : (s + 1) * P], src, ident[:])
+            m["gate_t", h] = gate_t[:].rearrange("w e n -> w n e")
 
-        def copy_gate(g):
-            c, part = divmod(g, GROUPS_PER_CHUNK)
-            mine = group_tiles[g]
-            if part == 0:
-                grad_sb = factors.tile([P, SLOTS * P], F32)
-                nc.scalar.copy(out=grad_sb[:], in_=chunk_tiles[c]["grad_words"][:])
-                chunk_tiles[c]["grad_sb"] = grad_sb
-            gate_sb = factors.tile([P, COLS, PAIR], F32)
-            nc.scalar.copy(out=gate_sb[:], in_=mine["gate_t"])
-            mine["gate_sb"] = gate_sb
-            grad_pairs = chunk_tiles[c]["grad_sb"][:, part * COLS : (part + 1) * COLS]
-            mine["grad_t"] = grad_pairs.bitcast(BF16).rearrange("w (n e) -> w n e", e=PAIR)
+        def copy_grad(c, h):
+            m = chunk[c]
+            if "left" not in m:
+                left = factors.tile([P, 2, SLOTS * P, PAIR], F32)
+                m["left"] = left
+            if by_py(c, h):
+                nc.scalar.copy(out=m["left"][:, 0, h * COLS : (h + 1) * COLS, :], in_=m["neg_gb", h][:].rearrange("w e n -> w n e"))
+            else:
+                grad_sb = factors.tile([P, COLS], F32)
+                nc.scalar.copy(out=grad_sb[:], in_=m["grad_words", h][:])
+                m["grad_t", h] = grad_sb[:].bitcast(BF16).rearrange("w (n e) -> w n e", e=PAIR)
 
-        def flip_right(g, s):
-            mine = group_tiles[g]
+        def flip_right(c, s):
+            m = chunk[c]
             right = right_banks.tile([P, 2, PAIR, P], F32)
-            upd_pairs = mine["upd_in"][:, s, :].rearrange("r (w e) -> r e w", e=PAIR)
             for e in range(PAIR):
-                nc.tensor.transpose(right[:, 0, e, :], mine["upd_sq"][:, s, e, :], ident[:])
+                nc.tensor.transpose(right[:, 0, e, :], m["upd_sq"][:, s, e, :], ident[:])
             for e in range(PAIR):
-                nc.tensor.matmul(
-                    out=right[:, 1, e, :], lhsT=upd_pairs[:, e, :], rhs=ident[:],
-                    start=True, stop=False, is_transpose=True,
-                )
-                nc.tensor.matmul(
-                    out=right[:, 1, e, :], lhsT=mine["neg_query"][:, s, e, :], rhs=ident[:],
-                    start=False, stop=True, is_transpose=True,
-                )
-            mine["right", s] = right
+                if c in ZC:
+                    ue = m["upd"][:, s, :].rearrange("r (w e) -> r e w", e=PAIR)
+                    nc.tensor.matmul(out=right[:, 1, e, :], lhsT=ue[:, e, :], rhs=ident[:], start=True, stop=False, is_transpose=True)
+                    nc.tensor.matmul(out=right[:, 1, e, :], lhsT=m["neg_query"][:, s, e, :], rhs=ident[:], start=False, stop=True, is_transpose=True)
+                else:
+                    nc.tensor.transpose(right[:, 1, e, :], m["diff"][:, s, e, :], ident[:])
+            m["right", s] = right
 
-        def first_left(g):
-            mine = group_tiles[g]
-            left = factors.tile([P, 2, COLS, PAIR], F32)
-            nc.vector.scalar_tensor_tensor(
-                out=left[:, 0, :, :], in0=mine["gate_t"], scalar=1.0, in1=mine["grad_t"],
-                op0=ALU.subtract, op1=ALU.mult,
-            )
-            mine["left"] = left
+        def first_left(c, h):
+            m = chunk[c]
+            cs = slice(h * COLS, (h + 1) * COLS)
+            if not by_py(c, h):
+                nc.vector.scalar_tensor_tensor(out=m["left"][:, 0, cs, :], in0=m["gate_t", h], scalar=1.0, in1=m["grad_t", h], op0=ALU.subtract, op1=ALU.mult)
 
-        def second_left(g):
-            mine = group_tiles[g]
-            left = mine["left"]
-            nc.gpsimd.tensor_tensor(
-                out=left[:, 1, :, :], in0=mine["gate_sb"][:], in1=left[:, 0, :, :], op=ALU.mult
-            )
+        def second_left(c, h):
+            m = chunk[c]
+            cs = slice(h * COLS, (h + 1) * COLS)
+            nc.vector.tensor_tensor(out=m["left"][:, 1, cs, :], in0=m["gate_t", h], in1=m["left"][:, 0, cs, :], op=ALU.mult)
 
-        def direct_term(g):
-            mine = group_tiles[g]
-            ga = direct.tile([P, GROUP, D], F32)
-            nc.gpsimd.tensor_tensor(out=ga[:], in0=mine["grad_in"], in1=mine["gate_in"], op=ALU.mult)
-            mine["ga"] = ga
+        def direct_term(c):
+            m = chunk[c]
+            ga = direct.tile([P, SLOTS, PAIR, P], F32)
+            for lo, hi in ((0, 2), (2, 4)) if c < TSMALL else ((0, 4),):
+                src = m["gate_de"][:, lo:hi] if AD and c >= ADMIN else de(m["gate"][:, lo:hi, :])
+                nc.gpsimd.tensor_tensor(out=ga[:, lo:hi], in0=de(m["grad"][:, lo:hi, :]), in1=src, op=ALU.mult)
+            m["ga"] = ga
 
-        def products(g, s):
-            c, part = divmod(g, GROUPS_PER_CHUNK)
-            mine = group_tiles[g]
-            if part == 0 and s == 0:
+        def difference(c):
+            m = chunk[c]
+            if c in ZC:
+                return
+            diff = diffs.tile([P, SLOTS, PAIR, P], F32)
+            for lo, hi in pieces(c):
+                nc.gpsimd.tensor_tensor(out=diff[:, lo:hi], in0=de(m["upd"][:, lo:hi, :]), in1=de(m["query"][:, lo:hi, :]), op=ALU.subtract)
+            m["diff"] = diff
+
+        def products(c, s):
+            m = chunk[c]
+            if "grouped" not in m:
                 grouped = packed.tile([P, SLOTS * P, PACK], BF16, align_bytes=64)
-                chunk_tiles[c]["grouped"] = grouped
-            slot = part * GROUP + s
+                m["grouped"] = grouped
+            cs = slice(s * P, (s + 1) * P)
             nc.vector.tensor_tensor(
-                out=chunk_tiles[c]["grouped"][:, slot * P : (slot + 1) * P, :].rearrange(
-                    "w n (b e) -> w n b e", e=PAIR
-                ),
-                in0=mine["right", s][:].rearrange("w b e n -> w n b e"),
-                in1=mine["left"][:, :, s * P : (s + 1) * P, :].rearrange("w b n e -> w n b e"),
+                out=m["grouped"][:, cs, :].rearrange("w n (b e) -> w n b e", e=PAIR),
+                in0=m["right", s][:].rearrange("w b e n -> w n b e"),
+                in1=m["left"][:, :, cs, :].rearrange("w b n e -> w n b e"),
                 op=ALU.mult,
             )
 
         def quantise(c):
-            mine = chunk_tiles[c]
+            m = chunk[c]
             dz_codes = packed.tile([P, SLOTS * P], U32, align_bytes=64)
             dz_scales = packed.tile([P, SLOTS * P], U8, align_bytes=64)
-            nc.vector.quantize_mx(
-                out=dz_codes[:].bitcast(E5M2X4),
-                scales=dz_scales[:],
-                in_=mine["grouped"][:].rearrange("w n t -> w (n t)"),
-            )
-            mine["codes"] = dz_codes
-            mine["scales"] = dz_scales
+            m["codes"] = dz_codes
+            m["scales"] = dz_scales
+            for lo, hi in ((0, 2), (2, 4)) if c == CHUNKS - 1 else ((0, 4),):
+                nc.vector.quantize_mx(out=dz_codes[:, lo * P : hi * P].bitcast(E5M2X4), scales=dz_scales[:, lo * P : hi * P], in_=m["grouped"][:, lo * P : hi * P, :].rearrange("w n t -> w (n t)"))
 
-        def multiply(c):
-            mine = chunk_tiles[c]
-            for part in range(GROUPS_PER_CHUNK):
+        def mx_pass(c, h, i, n):
+            m = chunk[c]
+            if i == 0:
                 acc = sums.tile([P, GROUP, D], F32)
-                for s in range(GROUP):
-                    tokens = slice((part * GROUP + s) * P, (part * GROUP + s + 1) * P)
-                    w_cols = slice(D - s * D, D - s * D + N_PASS)
-                    nc.tensor.matmul_mx(
-                        out=acc[:].rearrange("r s o -> r (s o)"),
-                        lhsT=mine["codes"][:, tokens].bitcast(E5M2X4),
-                        lhsT_scale=mine["scales"][:, tokens],
-                        rhs=w_codes[:, w_cols].bitcast(E4M3X4),
-                        rhs_scale=w_scales[:, w_cols],
-                        start=(s == 0),
-                        stop=(s == GROUP - 1),
-                    )
-                group_tiles[c * GROUPS_PER_CHUNK + part]["acc"] = acc
+                m["acc", h] = acc
+            s = 2 * h + min(i, 1)
+            tokens = slice(s * P, (s + 1) * P)
+            w0 = (N_PASS, D, 0, 0, 0, 0)[i]
+            nc.tensor.matmul_mx(
+                out=m["acc", h][:].rearrange("r s o -> r (s o)"),
+                lhsT=m["codes"][:, tokens].bitcast(E5M2X4), lhsT_scale=m["scales"][:, tokens],
+                rhs=w_codes[:, w0 : w0 + N_PASS].bitcast(E4M3X4), rhs_scale=w_scales[:, w0 : w0 + N_PASS],
+                start=(i == 0), stop=(i == n - 1),
+            )
 
-        def add_and_store(g):
-            ga = group_tiles[g]["ga"]
-            nc.vector.tensor_tensor(out=ga[:], in0=group_tiles[g]["acc"][:], in1=ga[:], op=ALU.add)
-            nc.sync.dma_start(out=out_v[:, g * GROUP : (g + 1) * GROUP, :], in_=ga[:])
+        def multiply(c, h):
+            for i in range(2):
+                mx_pass(c, h, i, 2)
 
-        def step(k):
-            c, part = divmod(k, GROUPS_PER_CHUNK)
-            if part == 0 and c + AHEAD < CHUNKS:
+        def add_and_store(c, h):
+            m = chunk[c]
+            sl = slice(h * GROUP, (h + 1) * GROUP)
+            result = results.tile([P, GROUP, D], F32)
+            nc.vector.tensor_tensor(
+                out=result[:].rearrange("r s (w e) -> r s w e", e=PAIR),
+                in0=m["acc", h][:].rearrange("r s (w e) -> r s w e", e=PAIR),
+                in1=m["ga"][:, sl].rearrange("r s e w -> r s w e"), op=ALU.add)
+            nc.sync.dma_start(out=out_v[:, c * SLOTS + h * GROUP : c * SLOTS + (h + 1) * GROUP, :], in_=result[:])
+
+        ok = lambda x: 0 <= x < CHUNKS
+
+        def scalar_prep(c):
+            for lo, hi in pieces(c):
+                if AD and c >= ADMIN:
+                    prep(c, "ad", lo, hi)
+                prep(c, "sq", lo, hi)
+                if lo == 0:
+                    prep(c, "ng", 0, 4)
+                prep(c, "m1", lo, hi)
+
+        def left_side(c):
+            m = chunk[c]
+            lead = 1 if by_py(c, 1) else 0
+            m["order"] = (lead, 1 - lead)
+            for h in range(2):
+                if not by_py(c, h):
+                    first_left(c, h)
+            for h in m["order"]:
+                second_left(c, h)
+
+        def flip_copy(c, h):
+            flip_gate(c, h)
+            flip_grad(c, h)
+            copy_grad(c, h)
+
+        def step(c):
+            if ok(c + AHEAD):
                 load(c + AHEAD)
-            if k + 1 < GROUPS:
-                flip_gate(k + 1)
-            if k < GROUPS:
-                flip_right(k, 0)
-                flip_right(k, 1)
-            if k + 2 < GROUPS:
-                square_and_negate(k + 2)
-            if k + 1 < GROUPS:
-                copy_gate(k + 1)
-            if k + 2 < GROUPS:
-                subtract_one(k + 2)
-            if 0 <= k - 4 < GROUPS:
-                add_and_store(k - 4)
-            if k < GROUPS:
-                first_left(k)
-            if part == 1 and 1 <= c <= CHUNKS:
+            if ok(c - 2):
+                add_and_store(c - 2, 0)
+                add_and_store(c - 2, 1)
+            if ok(c - 1):
                 quantise(c - 1)
-            if k < GROUPS:
-                second_left(k)
-                direct_term(k)
-            if 0 <= k - 1 < GROUPS:
-                products(k - 1, 0)
-                products(k - 1, 1)
-            if part == 1 and 1 <= c <= CHUNKS:
-                multiply(c - 1)
+            if ok(c + 1) and c >= 1:
+                direct_term(c + 1)
+                difference(c + 1)
+            if c == 0:
+                prep(1, "sq", 0, 4)
+                if 1 in ZC:
+                    prep(1, "nq", 0, 4)
+                prep(1, "m1", 0, 4)
+            elif ok(c + 2):
+                prep(c + 2, "ad", 0, 4)
+                prep(c + 2, "sq", 0, 4)
+            if ok(c):
+                lead = 1 if by_py(c, 1) else 0
+                sl = (2 * lead, 2 * lead + 1, 2 - 2 * lead, 3 - 2 * lead)
+                for s in sl[0:3]:
+                    flip_right(c, s)
+                left_side(c)
+            if ok(c - 1):
+                multiply(c - 1, 0)
+                if MSPLIT == 0:
+                    multiply(c - 1, 1)
+            if ok(c + 2) and c >= 1:
+                prep(c + 2, "ng", 0, 4)
+            if ok(c + 1):
+                flip_copy(c + 1, FIRST)
+            if ok(c + 2) and c >= 1:
+                prep(c + 2, "m1", 0, 4)
+            if ok(c):
+                products(c, sl[0])
+                flip_right(c, sl[3])
+            if ok(c - 1) and MSPLIT == 2:
+                mx_pass(c - 1, 1, 0, 2 + ZERO)
+                mx_pass(c - 1, 1, 1, 2 + ZERO)
+            if ok(c + 1):
+                flip_copy(c + 1, 1 - FIRST)
+            if ok(c - 1) and MSPLIT == 2:
+                for z in range(ZERO):
+                    mx_pass(c - 1, 1, 2 + z, 2 + ZERO)
+            if ok(c):
+                for s in sl[1:4]:
+                    products(c, s)
+            if c == 0:
+                if ADMIN <= 2:
+                    prep(2, "ad", 0, 4)
+                prep(2, "sq", 0, 4)
+                if 2 in ZC:
+                    prep(2, "nq", 0, 4)
+                prep(2, "m1", 0, 4)
 
         load(0)
         w_rows = const.tile([P, D // P, K], BF16)
-        nc.sync.dma_start(
-            out=w_rows[:, :, 0:D], in_=w_lin[0:D, :].rearrange("(h r) k -> r h k", r=P)
-        )
-        nc.sync.dma_start(
-            out=w_rows[:, :, D:K], in_=w_gate[0:D, :].rearrange("(h r) k -> r h k", r=P)
-        )
-        for c in range(1, AHEAD):
-            load(c)
+        nc.sync.dma_start(out=w_rows[:, :, 0:D], in_=w_lin[0:D, :].rearrange("(h r) k -> r h k", r=P))
+        nc.sync.dma_start(out=w_rows[:, :, D:K], in_=w_gate[0:D, :].rearrange("(h r) k -> r h k", r=P))
+        load(1)
+        load(2)
         ident = const.tile([P, P], F32)
         make_identity(nc, ident[:])
-        w_codes = const.tile([P, D + N_PASS], U32, align_bytes=64)
-        w_scales = const.tile([P, D + N_PASS], U8, align_bytes=64)
+        w_codes = const.tile([P, N_PASS + D + D], U32, align_bytes=64)
+        w_scales = const.tile([P, N_PASS + D + D], U8, align_bytes=64)
         nc.vector.memset(w_codes[:].bitcast(I32), 0)
         nc.vector.memset(w_scales[:].bitcast(I32), 0)
-        flip_gate(0)
-        copy_gate(0)
-        square_and_negate(0)
-        subtract_one(0)
-        square_and_negate(1)
-        subtract_one(1)
-        step(0)
-
+        for h in range(2):
+            flip_copy(0, h)
+        difference(0)
+        for lo, hi in pieces(0):
+            prep(0, "sq", lo, hi)
+            prep(0, "m1", lo, hi)
         w_bank = sums.tile([P, 2, D], F32, tag="acc")
         for b in range(2):
             for half in range(D // P):
-                nc.tensor.transpose(
-                    w_bank[:, b, half * P : (half + 1) * P],
-                    w_rows[:, half, b * D : (b + 1) * D].bitcast(F32),
-                    ident[:],
-                )
+                nc.tensor.transpose(w_bank[:, b, half * P : (half + 1) * P], w_rows[:, half, b * D : (b + 1) * D].bitcast(F32), ident[:])
         w_grouped = const.tile([P, D * PACK], BF16, align_bytes=64)
-        nc.scalar.copy(
-            out=w_grouped[:].bitcast(F32).rearrange("w (o b) -> w o b", b=2),
-            in_=w_bank[:].rearrange("w b o -> w o b"),
-        )
-        step(1)
-        nc.vector.quantize_mx(
-            out=w_codes[:, D : 2 * D].bitcast(E4M3X4),
-            scales=w_scales[:, D : 2 * D],
-            in_=w_grouped[:],
-        )
-
-        for k in range(2, GROUPS + 4):
-            step(k)
+        nc.scalar.copy(out=w_grouped[:].bitcast(F32).rearrange("w (o b) -> w o b", b=2), in_=w_bank[:].rearrange("w b o -> w o b"))
+        difference(1)
+        direct_term(0)
+        direct_term(1)
+        step(0)
+        nc.vector.quantize_mx(out=w_codes[:, N_PASS : N_PASS + D].bitcast(E4M3X4), scales=w_scales[:, N_PASS : N_PASS + D], in_=w_grouped[:])
+        for c in range(1, CHUNKS + 2):
+            step(c)

@@ -27,16 +27,15 @@ GROUPS_PER_CHUNK = SLOTS // GROUP
 COLS = GROUP * P
 N_PASS = 512
 AHEAD = 3
-ZERO = 0
 TBUFS = 3
 YSET = (1, 3)
 AD = 1
+FLO = 0
+FHI = 16
+FS = (0,)
 ADMIN = 3
 PYMIN = 3
-ZC = (1, 2)
-TSMALL = 2
-G0 = 0
-MSPLIT = 2
+ZC = (1,)
 FIRST = 0
 FLOPS = 2 * TOKENS * K * D
 BYTES = TOKENS * D * (2 + 4 + 4 + 2 + 4) + 2 * D * D * 2
@@ -56,7 +55,7 @@ def tile_scan_pb_t_v_kernel(
 
     with ExitStack() as stack:
         const = stack.enter_context(tc.tile_pool(name="const", bufs=1))
-        inputs = stack.enter_context(tc.tile_pool(name="inputs", bufs=6))
+        inputs = stack.enter_context(tc.tile_pool(name="inputs", bufs=5))
         prepared = stack.enter_context(tc.tile_pool(name="prepared", bufs=4))
         factors = stack.enter_context(tc.tile_pool(name="factors", bufs=3))
         packed = stack.enter_context(tc.tile_pool(name="packed", bufs=3))
@@ -66,6 +65,7 @@ def tile_scan_pb_t_v_kernel(
         right_banks = stack.enter_context(tc.psum_pool(name="right_banks", bufs=3))
         sums = stack.enter_context(tc.psum_pool(name="sums", bufs=2))
         stack.enter_context(tc.manual_schedule())
+        negq = stack.enter_context(tc.tile_pool(name="negq", bufs=2))
         diffs = stack.enter_context(tc.tile_pool(name="diffs", bufs=2))
         results = stack.enter_context(tc.tile_pool(name="results", bufs=4))
         chunk = {}
@@ -76,9 +76,10 @@ def tile_scan_pb_t_v_kernel(
             upd_in = inputs.tile([P, SLOTS, D], F32)
             query_in = inputs.tile([P, SLOTS, D], BF16)
             parts = ((0, 2), (2, 4)) if c < 1 else ((0, 4),)
-            for lo, hi in parts:
-                for t, v in ((grad_in, grad_v), (gate_in, gate_v), (upd_in, upd_v), (query_in, query_v)):
-                    nc.sync.dma_start(out=t[:, lo:hi, :], in_=v[:, c * SLOTS + lo : c * SLOTS + hi, :])
+            for pair in (((grad_in, grad_v), (gate_in, gate_v)), ((upd_in, upd_v), (query_in, query_v))):
+                for lo, hi in parts:
+                    for t, v in pair:
+                        nc.sync.dma_start(out=t[:, lo:hi, :], in_=v[:, c * SLOTS + lo : c * SLOTS + hi, :])
             chunk[c] = {"gate": gate_in, "grad": grad_in, "upd": upd_in, "query": query_in}
 
         def pieces(c):
@@ -86,6 +87,9 @@ def tile_scan_pb_t_v_kernel(
 
         def de(ap):
             return ap.rearrange("r s (w e) -> r s e w", e=PAIR)
+
+        def zn(c):
+            return 4 if c in ZC else 0
 
         def by_py(c, h):
             return (2 * c + h) % 4 in YSET and c >= PYMIN
@@ -106,9 +110,12 @@ def tile_scan_pb_t_v_kernel(
                         if by_py(c, h):
                             nc.scalar.activation(out=neg_grad[:, 2 * h : 2 * h + 2], in_=de(m["grad"][:, 2 * h : 2 * h + 2, :]), func=ACT.Copy, scale=-1.0)
             elif what == "nq":
-                neg_query = prepared.tile([P, SLOTS, PAIR, P], F32)
+                k = zn(c)
+                if k == 0:
+                    return
+                neg_query = negq.tile([P, SLOTS, PAIR, P], F32)
                 m["neg_query"] = neg_query
-                nc.scalar.activation(out=neg_query[:], in_=de(m["query"][:]), func=ACT.Copy, scale=-1.0)
+                nc.scalar.activation(out=neg_query[:, 0:k], in_=de(m["query"][:, 0:k, :]), func=ACT.Copy, scale=-1.0)
             elif what == "ad":
                 if lo == 0:
                     gate_de = prepared.tile([P, SLOTS, PAIR, P], F32)
@@ -161,9 +168,12 @@ def tile_scan_pb_t_v_kernel(
             m = chunk[c]
             right = right_banks.tile([P, 2, PAIR, P], F32)
             for e in range(PAIR):
-                nc.tensor.transpose(right[:, 0, e, :], m["upd_sq"][:, s, e, :], ident[:])
+                if FLO <= c < FHI and s in FS:
+                    nc.tensor.matmul(out=right[:, 0, e, :], lhsT=m["upd_sq"][:, s, e, :], rhs=ident[:], start=True, stop=True)
+                else:
+                    nc.tensor.transpose(right[:, 0, e, :], m["upd_sq"][:, s, e, :], ident[:])
             for e in range(PAIR):
-                if c in ZC:
+                if s < zn(c):
                     ue = m["upd"][:, s, :].rearrange("r (w e) -> r e w", e=PAIR)
                     nc.tensor.matmul(out=right[:, 1, e, :], lhsT=ue[:, e, :], rhs=ident[:], start=True, stop=False, is_transpose=True)
                     nc.tensor.matmul(out=right[:, 1, e, :], lhsT=m["neg_query"][:, s, e, :], rhs=ident[:], start=False, stop=True, is_transpose=True)
@@ -184,18 +194,21 @@ def tile_scan_pb_t_v_kernel(
 
         def direct_term(c):
             m = chunk[c]
-            ga = direct.tile([P, SLOTS, PAIR, P], F32)
-            for lo, hi in ((0, 2), (2, 4)) if c < TSMALL else ((0, 4),):
+            if "ga" not in m:
+                ga = direct.tile([P, SLOTS, PAIR, P], F32)
+                m["ga"] = ga
+            ga = m["ga"]
+            for lo, hi in ((0, 4),):
                 src = m["gate_de"][:, lo:hi] if AD and c >= ADMIN else de(m["gate"][:, lo:hi, :])
                 nc.gpsimd.tensor_tensor(out=ga[:, lo:hi], in0=de(m["grad"][:, lo:hi, :]), in1=src, op=ALU.mult)
-            m["ga"] = ga
 
         def difference(c):
             m = chunk[c]
-            if c in ZC:
+            if zn(c) == 4:
                 return
             diff = diffs.tile([P, SLOTS, PAIR, P], F32)
             for lo, hi in pieces(c):
+                lo = max(lo, zn(c))
                 nc.gpsimd.tensor_tensor(out=diff[:, lo:hi], in0=de(m["upd"][:, lo:hi, :]), in1=de(m["query"][:, lo:hi, :]), op=ALU.subtract)
             m["diff"] = diff
 
@@ -212,14 +225,19 @@ def tile_scan_pb_t_v_kernel(
                 op=ALU.mult,
             )
 
-        def quantise(c):
+        def quantise(c, lo=0, hi=SLOTS):
             m = chunk[c]
-            dz_codes = packed.tile([P, SLOTS * P], U32, align_bytes=64)
-            dz_scales = packed.tile([P, SLOTS * P], U8, align_bytes=64)
-            m["codes"] = dz_codes
-            m["scales"] = dz_scales
-            for lo, hi in ((0, 2), (2, 4)) if c == CHUNKS - 1 else ((0, 4),):
-                nc.vector.quantize_mx(out=dz_codes[:, lo * P : hi * P].bitcast(E5M2X4), scales=dz_scales[:, lo * P : hi * P], in_=m["grouped"][:, lo * P : hi * P, :].rearrange("w n t -> w (n t)"))
+            if "codes" not in m:
+                dz_codes = packed.tile([P, SLOTS * P], U32, align_bytes=64)
+                dz_scales = packed.tile([P, SLOTS * P], U8, align_bytes=64)
+                m["codes"] = dz_codes
+                m["scales"] = dz_scales
+            cols = slice(lo * P, hi * P)
+            nc.vector.quantize_mx(
+                out=m["codes"][:, cols].bitcast(E5M2X4),
+                scales=m["scales"][:, cols],
+                in_=m["grouped"][:, cols, :].rearrange("w n t -> w (n t)"),
+            )
 
         def mx_pass(c, h, i, n):
             m = chunk[c]
@@ -285,13 +303,14 @@ def tile_scan_pb_t_v_kernel(
             if ok(c - 1):
                 quantise(c - 1)
             if ok(c + 1) and c >= 1:
-                direct_term(c + 1)
+                for j in (1, 2) if c == 1 else (c + 1,):
+                    ga = direct.tile([P, SLOTS, PAIR, P], F32)
+                    chunk[j]["ga"] = ga
+                    nc.vector.memset(ga[:, 0, 0, 0:1], 0.0)
+                    direct_term(j)
                 difference(c + 1)
             if c == 0:
                 prep(1, "sq", 0, 4)
-                if 1 in ZC:
-                    prep(1, "nq", 0, 4)
-                prep(1, "m1", 0, 4)
             elif ok(c + 2):
                 prep(c + 2, "ad", 0, 4)
                 prep(c + 2, "sq", 0, 4)
@@ -303,25 +322,24 @@ def tile_scan_pb_t_v_kernel(
                 left_side(c)
             if ok(c - 1):
                 multiply(c - 1, 0)
-                if MSPLIT == 0:
-                    multiply(c - 1, 1)
             if ok(c + 2) and c >= 1:
                 prep(c + 2, "ng", 0, 4)
+                prep(c + 2, "nq", 0, 4)
             if ok(c + 1):
                 flip_copy(c + 1, FIRST)
+            if c == 0:
+                prep(1, "nq", 0, 4)
             if ok(c + 2) and c >= 1:
                 prep(c + 2, "m1", 0, 4)
             if ok(c):
                 products(c, sl[0])
                 flip_right(c, sl[3])
-            if ok(c - 1) and MSPLIT == 2:
-                mx_pass(c - 1, 1, 0, 2 + ZERO)
-                mx_pass(c - 1, 1, 1, 2 + ZERO)
+            if ok(c - 1):
+                multiply(c - 1, 1)
             if ok(c + 1):
                 flip_copy(c + 1, 1 - FIRST)
-            if ok(c - 1) and MSPLIT == 2:
-                for z in range(ZERO):
-                    mx_pass(c - 1, 1, 2 + z, 2 + ZERO)
+            if c == 0:
+                prep(1, "m1", 0, 4)
             if ok(c):
                 for s in sl[1:4]:
                     products(c, s)
@@ -333,10 +351,10 @@ def tile_scan_pb_t_v_kernel(
                     prep(2, "nq", 0, 4)
                 prep(2, "m1", 0, 4)
 
-        load(0)
         w_rows = const.tile([P, D // P, K], BF16)
         nc.sync.dma_start(out=w_rows[:, :, 0:D], in_=w_lin[0:D, :].rearrange("(h r) k -> r h k", r=P))
         nc.sync.dma_start(out=w_rows[:, :, D:K], in_=w_gate[0:D, :].rearrange("(h r) k -> r h k", r=P))
+        load(0)
         load(1)
         load(2)
         ident = const.tile([P, P], F32)
@@ -345,22 +363,33 @@ def tile_scan_pb_t_v_kernel(
         w_scales = const.tile([P, N_PASS + D + D], U8, align_bytes=64)
         nc.vector.memset(w_codes[:].bitcast(I32), 0)
         nc.vector.memset(w_scales[:].bitcast(I32), 0)
-        for h in range(2):
-            flip_copy(0, h)
-        difference(0)
-        for lo, hi in pieces(0):
-            prep(0, "sq", lo, hi)
-            prep(0, "m1", lo, hi)
         w_bank = sums.tile([P, 2, D], F32, tag="acc")
         for b in range(2):
             for half in range(D // P):
                 nc.tensor.transpose(w_bank[:, b, half * P : (half + 1) * P], w_rows[:, half, b * D : (b + 1) * D].bitcast(F32), ident[:])
         w_grouped = const.tile([P, D * PACK], BF16, align_bytes=64)
         nc.scalar.copy(out=w_grouped[:].bitcast(F32).rearrange("w (o b) -> w o b", b=2), in_=w_bank[:].rearrange("w b o -> w o b"))
+        flip_grad(0, 0)
+        copy_grad(0, 0)
+        nc.vector.quantize_mx(out=w_codes[:, N_PASS : N_PASS + D].bitcast(E4M3X4), scales=w_scales[:, N_PASS : N_PASS + D], in_=w_grouped[:])
+        flip_gate(0, 0)
+        flip_grad(0, 1)
+        copy_grad(0, 1)
+        flip_gate(0, 1)
+        difference(0)
+        for lo, hi in pieces(0):
+            prep(0, "sq", lo, hi)
+            prep(0, "m1", lo, hi)
         difference(1)
         direct_term(0)
-        direct_term(1)
-        step(0)
-        nc.vector.quantize_mx(out=w_codes[:, N_PASS : N_PASS + D].bitcast(E4M3X4), scales=w_scales[:, N_PASS : N_PASS + D], in_=w_grouped[:])
-        for c in range(1, CHUNKS + 2):
+        for c in range(CHUNKS):
             step(c)
+        last = CHUNKS - 1
+        quantise(last, GROUP, SLOTS)
+        add_and_store(last - 1, 0)
+        quantise(last, 0, GROUP)
+        add_and_store(last - 1, 1)
+        for h in (1, 0):
+            multiply(last, h)
+        for h in (1, 0):
+            add_and_store(last, h)

@@ -30,9 +30,8 @@ AHEAD = 3
 TBUFS = 3
 YSET = (1, 3)
 AD = 1
-FLO = 0
-FHI = 16
-FS = (0,)
+ZA = 1
+ZB = 1
 ADMIN = 3
 PYMIN = 3
 ZC = (1,)
@@ -168,10 +167,7 @@ def tile_scan_pb_t_v_kernel(
             m = chunk[c]
             right = right_banks.tile([P, 2, PAIR, P], F32)
             for e in range(PAIR):
-                if FLO <= c < FHI and s in FS:
-                    nc.tensor.matmul(out=right[:, 0, e, :], lhsT=m["upd_sq"][:, s, e, :], rhs=ident[:], start=True, stop=True)
-                else:
-                    nc.tensor.transpose(right[:, 0, e, :], m["upd_sq"][:, s, e, :], ident[:])
+                nc.tensor.transpose(right[:, 0, e, :], m["upd_sq"][:, s, e, :], ident[:])
             for e in range(PAIR):
                 if s < zn(c):
                     ue = m["upd"][:, s, :].rearrange("r (w e) -> r e w", e=PAIR)
@@ -255,8 +251,9 @@ def tile_scan_pb_t_v_kernel(
             )
 
         def multiply(c, h):
-            for i in range(2):
-                mx_pass(c, h, i, 2)
+            n = (ZA, ZB)[h]
+            for i in range(2 + n):
+                mx_pass(c, h, i, 2 + n)
 
         def add_and_store(c, h):
             m = chunk[c]

@@ -29,9 +29,6 @@ N_PASS = 512
 AHEAD = 3
 TBUFS = 3
 YSET = (1, 3)
-AD = 1
-ZA = 1
-ZB = 1
 ADMIN = 3
 PYMIN = 3
 ZC = (1,)
@@ -144,7 +141,7 @@ def tile_scan_pb_t_v_kernel(
             gate_t = gate_banks.tile([P, PAIR, COLS], F32)
             for s in range(GROUP):
                 for e in range(PAIR):
-                    if AD and c >= ADMIN:
+                    if c >= ADMIN:
                         src = m["gate_de"][:, h * GROUP + s, e, :]
                     else:
                         src = m["gate"][:, h * GROUP + s, :].rearrange("r (w e) -> r e w", e=PAIR)[:, e, :]
@@ -195,7 +192,7 @@ def tile_scan_pb_t_v_kernel(
                 m["ga"] = ga
             ga = m["ga"]
             for lo, hi in ((0, 4),):
-                src = m["gate_de"][:, lo:hi] if AD and c >= ADMIN else de(m["gate"][:, lo:hi, :])
+                src = m["gate_de"][:, lo:hi] if c >= ADMIN else de(m["gate"][:, lo:hi, :])
                 nc.gpsimd.tensor_tensor(out=ga[:, lo:hi], in0=de(m["grad"][:, lo:hi, :]), in1=src, op=ALU.mult)
 
         def difference(c):
@@ -251,9 +248,8 @@ def tile_scan_pb_t_v_kernel(
             )
 
         def multiply(c, h):
-            n = (ZA, ZB)[h]
-            for i in range(2 + n):
-                mx_pass(c, h, i, 2 + n)
+            for i in range(2):
+                mx_pass(c, h, i, 2)
 
         def add_and_store(c, h):
             m = chunk[c]
@@ -269,7 +265,7 @@ def tile_scan_pb_t_v_kernel(
 
         def scalar_prep(c):
             for lo, hi in pieces(c):
-                if AD and c >= ADMIN:
+                if c >= ADMIN:
                     prep(c, "ad", lo, hi)
                 prep(c, "sq", lo, hi)
                 if lo == 0:
@@ -303,7 +299,8 @@ def tile_scan_pb_t_v_kernel(
                 for j in (1, 2) if c == 1 else (c + 1,):
                     ga = direct.tile([P, SLOTS, PAIR, P], F32)
                     chunk[j]["ga"] = ga
-                    nc.vector.memset(ga[:, 0, 0, 0:1], 0.0)
+                    if c == 1:
+                        nc.vector.memset(ga[:, 0, 0, 0:1], 0.0)
                     direct_term(j)
                 difference(c + 1)
             if c == 0:

@@ -311,11 +311,13 @@ def tile_scan_pb_t_v_kernel(
             if ok(c):
                 lead = 1 if by_py(c, 1) else 0
                 sl = (2 * lead, 2 * lead + 1, 2 - 2 * lead, 3 - 2 * lead)
-                for s in sl[0:3]:
-                    flip_right(c, s)
-                left_side(c)
+                flip_right(c, sl[0])
+                flip_right(c, sl[1])
             if ok(c - 1):
                 multiply(c - 1, 0)
+            if ok(c):
+                flip_right(c, sl[2])
+                left_side(c)
             if ok(c + 2) and c >= 1:
                 prep(c + 2, "ng", 0, 4)
                 prep(c + 2, "nq", 0, 4)

@@ -29,9 +29,9 @@ N_PASS = 512
 AHEAD = 3
 TBUFS = 3
 YSET = (1, 3)
-ADMIN = 3
+ADMIN = 4
 PYMIN = 3
-ZC = (1,)
+
 FIRST = 0
 FLOPS = 2 * TOKENS * K * D
 BYTES = TOKENS * D * (2 + 4 + 4 + 2 + 4) + 2 * D * D * 2
@@ -78,6 +78,26 @@ def tile_scan_pb_t_v_kernel(
                         nc.sync.dma_start(out=t[:, lo:hi, :], in_=v[:, c * SLOTS + lo : c * SLOTS + hi, :])
             chunk[c] = {"gate": gate_in, "grad": grad_in, "upd": upd_in, "query": query_in}
 
+        def load_piece(c, lo, hi):
+            m = chunk[c]
+            for name, v in (("grad", grad_v), ("gate", gate_v), ("upd", upd_v), ("query", query_v)):
+                nc.sync.dma_start(out=m[name][:, lo:hi, :], in_=v[:, c * SLOTS + lo : c * SLOTS + hi, :])
+
+        def load_first():
+            gate_in = inputs.tile([P, SLOTS, D], F32)
+            grad_in = inputs.tile([P, SLOTS, D], BF16)
+            upd_in = inputs.tile([P, SLOTS, D], F32)
+            query_in = inputs.tile([P, SLOTS, D], BF16)
+            chunk[0] = {"gate": gate_in, "grad": grad_in, "upd": upd_in, "query": query_in}
+            load_piece(0, 0, 2)
+
+        def load_second():
+            load_piece(0, 2, 4)
+
+        def vminus(c, lo, hi):
+            sq = chunk[c]["upd_sq"][:, lo:hi]
+            nc.vector.tensor_scalar(out=sq, in0=sq, scalar1=-1.0, scalar2=None, op0=ALU.add)
+
         def pieces(c):
             return ((0, 2), (2, 4)) if c < 1 else ((0, 4),)
 
@@ -85,7 +105,7 @@ def tile_scan_pb_t_v_kernel(
             return ap.rearrange("r s (w e) -> r s e w", e=PAIR)
 
         def zn(c):
-            return 4 if c in ZC else 0
+            return {2: 2, 3: 1}.get(c, 0)
 
         def by_py(c, h):
             return (2 * c + h) % 4 in YSET and c >= PYMIN
@@ -113,6 +133,8 @@ def tile_scan_pb_t_v_kernel(
                 m["neg_query"] = neg_query
                 nc.scalar.activation(out=neg_query[:, 0:k], in_=de(m["query"][:, 0:k, :]), func=ACT.Copy, scale=-1.0)
             elif what == "ad":
+                if c < ADMIN:
+                    return
                 if lo == 0:
                     gate_de = prepared.tile([P, SLOTS, PAIR, P], F32)
                     m["gate_de"] = gate_de
@@ -197,12 +219,17 @@ def tile_scan_pb_t_v_kernel(
 
         def difference(c):
             m = chunk[c]
-            if zn(c) == 4:
-                return
             diff = diffs.tile([P, SLOTS, PAIR, P], F32)
             for lo, hi in pieces(c):
                 lo = max(lo, zn(c))
                 nc.gpsimd.tensor_tensor(out=diff[:, lo:hi], in0=de(m["upd"][:, lo:hi, :]), in1=de(m["query"][:, lo:hi, :]), op=ALU.subtract)
+            m["diff"] = diff
+
+        def difference_v(c):
+            m = chunk[c]
+            diff = diffs.tile([P, SLOTS, PAIR, P], F32)
+            for lo, hi in ((0, 2), (2, 4)):
+                nc.vector.tensor_tensor(out=diff[:, lo:hi], in0=de(m["upd"][:, lo:hi, :]), in1=de(m["query"][:, lo:hi, :]), op=ALU.subtract)
             m["diff"] = diff
 
         def products(c, s):
@@ -317,17 +344,21 @@ def tile_scan_pb_t_v_kernel(
                 multiply(c - 1, 0)
             if ok(c):
                 flip_right(c, sl[2])
-                left_side(c)
+                if c > 0:
+                    left_side(c)
             if ok(c + 2) and c >= 1:
                 prep(c + 2, "ng", 0, 4)
                 prep(c + 2, "nq", 0, 4)
+            if c == 0:
+                products(c, sl[0])
+                flip_right(c, sl[3])
             if ok(c + 1):
                 flip_copy(c + 1, FIRST)
             if c == 0:
                 prep(1, "nq", 0, 4)
             if ok(c + 2) and c >= 1:
                 prep(c + 2, "m1", 0, 4)
-            if ok(c):
+            if ok(c) and c > 0:
                 products(c, sl[0])
                 flip_right(c, sl[3])
             if ok(c - 1):
@@ -340,17 +371,20 @@ def tile_scan_pb_t_v_kernel(
                 for s in sl[1:4]:
                     products(c, s)
             if c == 0:
+                difference_v(1)
+                nc.vector.quantize_mx(out=w_codes[:, N_PASS : N_PASS + D].bitcast(E4M3X4), scales=w_scales[:, N_PASS : N_PASS + D], in_=w_grouped[:])
                 if ADMIN <= 2:
                     prep(2, "ad", 0, 4)
                 prep(2, "sq", 0, 4)
-                if 2 in ZC:
+                if zn(2):
                     prep(2, "nq", 0, 4)
                 prep(2, "m1", 0, 4)
 
         w_rows = const.tile([P, D // P, K], BF16)
+        load_first()
+        load_second()
         nc.sync.dma_start(out=w_rows[:, :, 0:D], in_=w_lin[0:D, :].rearrange("(h r) k -> r h k", r=P))
         nc.sync.dma_start(out=w_rows[:, :, D:K], in_=w_gate[0:D, :].rearrange("(h r) k -> r h k", r=P))
-        load(0)
         load(1)
         load(2)
         ident = const.tile([P, P], F32)
@@ -359,24 +393,27 @@ def tile_scan_pb_t_v_kernel(
         w_scales = const.tile([P, N_PASS + D + D], U8, align_bytes=64)
         nc.vector.memset(w_codes[:].bitcast(I32), 0)
         nc.vector.memset(w_scales[:].bitcast(I32), 0)
+        flip_grad(0, 0)
+        copy_grad(0, 0)
+        flip_gate(0, 0)
+        prep(0, "sq", 0, 2)
+        difference(0)
+        first_left(0, 0)
+        vminus(0, 0, 2)
+        second_left(0, 0)
+        flip_grad(0, 1)
+        copy_grad(0, 1)
+        flip_gate(0, 1)
+        prep(0, "sq", 2, 4)
+        prep(0, "m1", 2, 4)
         w_bank = sums.tile([P, 2, D], F32, tag="acc")
         for b in range(2):
             for half in range(D // P):
                 nc.tensor.transpose(w_bank[:, b, half * P : (half + 1) * P], w_rows[:, half, b * D : (b + 1) * D].bitcast(F32), ident[:])
         w_grouped = const.tile([P, D * PACK], BF16, align_bytes=64)
         nc.scalar.copy(out=w_grouped[:].bitcast(F32).rearrange("w (o b) -> w o b", b=2), in_=w_bank[:].rearrange("w b o -> w o b"))
-        flip_grad(0, 0)
-        copy_grad(0, 0)
-        nc.vector.quantize_mx(out=w_codes[:, N_PASS : N_PASS + D].bitcast(E4M3X4), scales=w_scales[:, N_PASS : N_PASS + D], in_=w_grouped[:])
-        flip_gate(0, 0)
-        flip_grad(0, 1)
-        copy_grad(0, 1)
-        flip_gate(0, 1)
-        difference(0)
-        for lo, hi in pieces(0):
-            prep(0, "sq", lo, hi)
-            prep(0, "m1", lo, hi)
-        difference(1)
+        first_left(0, 1)
+        second_left(0, 1)
         direct_term(0)
         for c in range(CHUNKS):
             step(c)

@@ -105,7 +105,7 @@ def tile_scan_pb_t_v_kernel(
             return ap.rearrange("r s (w e) -> r s e w", e=PAIR)
 
         def zn(c):
-            return {2: 2, 3: 1}.get(c, 0)
+            return {2: 2}.get(c, 0)
 
         def by_py(c, h):
             return (2 * c + h) % 4 in YSET and c >= PYMIN
@@ -262,7 +262,10 @@ def tile_scan_pb_t_v_kernel(
         def mx_pass(c, h, i, n):
             m = chunk[c]
             if i == 0:
-                acc = sums.tile([P, GROUP, D], F32)
+                if c == CHUNKS - 1:
+                    acc = right_banks.tile([P, GROUP, D], F32, tag="right")
+                else:
+                    acc = sums.tile([P, GROUP, D], F32, tag="acc")
                 m["acc", h] = acc
             s = 2 * h + min(i, 1)
             tokens = slice(s * P, (s + 1) * P)
@@ -278,14 +281,26 @@ def tile_scan_pb_t_v_kernel(
             for i in range(2):
                 mx_pass(c, h, i, 2)
 
-        def add_and_store(c, h):
+        def add_and_store(c, h, step=GROUP):
             m = chunk[c]
-            sl = slice(h * GROUP, (h + 1) * GROUP)
             result = results.tile([P, GROUP, D], F32)
-            nc.vector.tensor_tensor(
-                out=result[:].rearrange("r s (w e) -> r s w e", e=PAIR),
-                in0=m["acc", h][:].rearrange("r s (w e) -> r s w e", e=PAIR),
-                in1=m["ga"][:, sl].rearrange("r s e w -> r s w e"), op=ALU.add)
+            for lo in range(0, GROUP, step):
+                part = slice(lo, lo + step)
+                slots = slice(h * GROUP + lo, h * GROUP + lo + step)
+                nc.vector.tensor_tensor(
+                    out=result[:, part].rearrange("r s (w e) -> r s w e", e=PAIR),
+                    in0=m["acc", h][:, part].rearrange("r s (w e) -> r s w e", e=PAIR),
+                    in1=m["ga"][:, slots].rearrange("r s e w -> r s w e"), op=ALU.add)
+                nc.sync.dma_start(out=out_v[:, c * SLOTS + slots.start : c * SLOTS + slots.stop, :], in_=result[:, part])
+
+        def add_on_pool(c, h):
+            m = chunk[c]
+            result = results.tile([P, GROUP, D], F32)
+            nc.scalar.copy(out=result[:], in_=m["acc", h][:])
+            words = result[:].rearrange("r s (w e) -> r s w e", e=PAIR)
+            nc.gpsimd.tensor_tensor(
+                out=words, in0=words,
+                in1=m["ga"][:, h * GROUP : (h + 1) * GROUP].rearrange("r s e w -> r s w e"), op=ALU.add)
             nc.sync.dma_start(out=out_v[:, c * SLOTS + h * GROUP : c * SLOTS + (h + 1) * GROUP, :], in_=result[:])
 
         ok = lambda x: 0 <= x < CHUNKS
@@ -346,6 +361,8 @@ def tile_scan_pb_t_v_kernel(
                 flip_right(c, sl[2])
                 if c > 0:
                     left_side(c)
+            if c == CHUNKS - 1:
+                add_on_pool(c - 1, 0)
             if ok(c + 2) and c >= 1:
                 prep(c + 2, "ng", 0, 4)
                 prep(c + 2, "nq", 0, 4)
@@ -369,6 +386,8 @@ def tile_scan_pb_t_v_kernel(
                 prep(1, "m1", 0, 4)
             if ok(c):
                 for s in sl[1:4]:
+                    if s == sl[3] and c == CHUNKS - 1:
+                        quantise(c, sl[0], sl[0] + GROUP)
                     products(c, s)
             if c == 0:
                 difference_v(1)
@@ -418,11 +437,9 @@ def tile_scan_pb_t_v_kernel(
         for c in range(CHUNKS):
             step(c)
         last = CHUNKS - 1
-        quantise(last, GROUP, SLOTS)
-        add_and_store(last - 1, 0)
+        multiply(last, 1)
         quantise(last, 0, GROUP)
+        multiply(last, 0)
         add_and_store(last - 1, 1)
-        for h in (1, 0):
-            multiply(last, h)
-        for h in (1, 0):
-            add_and_store(last, h)
+        add_and_store(last, 1)
+        add_and_store(last, 0, 1)

@@ -28,8 +28,7 @@ COLS = GROUP * P
 N_PASS = 512
 AHEAD = 3
 TBUFS = 3
-YSET = (1, 3)
-ADMIN = 4
+ADMIN = 99
 PYMIN = 3
 
 FIRST = 0
@@ -72,7 +71,7 @@ def tile_scan_pb_t_v_kernel(
             upd_in = inputs.tile([P, SLOTS, D], F32)
             query_in = inputs.tile([P, SLOTS, D], BF16)
             parts = ((0, 2), (2, 4)) if c < 1 else ((0, 4),)
-            for pair in (((grad_in, grad_v), (gate_in, gate_v)), ((upd_in, upd_v), (query_in, query_v))):
+            for pair in (((upd_in, upd_v), (query_in, query_v)), ((grad_in, grad_v), (gate_in, gate_v))):
                 for lo, hi in parts:
                     for t, v in pair:
                         nc.sync.dma_start(out=t[:, lo:hi, :], in_=v[:, c * SLOTS + lo : c * SLOTS + hi, :])
@@ -105,10 +104,10 @@ def tile_scan_pb_t_v_kernel(
             return ap.rearrange("r s (w e) -> r s e w", e=PAIR)
 
         def zn(c):
-            return {2: 2}.get(c, 0)
+            return {2: 2}.get(c, 1 if c > 3 else 0)
 
         def by_py(c, h):
-            return (2 * c + h) % 4 in YSET and c >= PYMIN
+            return c >= PYMIN and (h == 1 or 2 < c < CHUNKS - 1)
 
         def prep(c, what, lo, hi):
             m = chunk[c]
@@ -213,7 +212,7 @@ def tile_scan_pb_t_v_kernel(
                 ga = direct.tile([P, SLOTS, PAIR, P], F32)
                 m["ga"] = ga
             ga = m["ga"]
-            for lo, hi in ((0, 4),):
+            for lo, hi in ((0, 2), (2, 4)) if by_py(c, 0) else ((0, 4),):
                 src = m["gate_de"][:, lo:hi] if c >= ADMIN else de(m["gate"][:, lo:hi, :])
                 nc.gpsimd.tensor_tensor(out=ga[:, lo:hi], in0=de(m["grad"][:, lo:hi, :]), in1=src, op=ALU.mult)
 
@@ -316,7 +315,7 @@ def tile_scan_pb_t_v_kernel(
 
         def left_side(c):
             m = chunk[c]
-            lead = 1 if by_py(c, 1) else 0
+            lead = 1 if by_py(c, 1) and not by_py(c, 0) else 0
             m["order"] = (lead, 1 - lead)
             for h in range(2):
                 if not by_py(c, h):
@@ -334,10 +333,11 @@ def tile_scan_pb_t_v_kernel(
                 load(c + AHEAD)
             if ok(c - 2):
                 add_and_store(c - 2, 0)
+            if ok(c - 2):
                 add_and_store(c - 2, 1)
             if ok(c - 1):
                 quantise(c - 1)
-            if ok(c + 1) and c >= 1:
+            if ok(c + 1):
                 for j in (1, 2) if c == 1 else (c + 1,):
                     ga = direct.tile([P, SLOTS, PAIR, P], F32)
                     chunk[j]["ga"] = ga
@@ -345,59 +345,49 @@ def tile_scan_pb_t_v_kernel(
                         nc.vector.memset(ga[:, 0, 0, 0:1], 0.0)
                     direct_term(j)
                 difference(c + 1)
-            if c == 0:
-                prep(1, "sq", 0, 4)
-            elif ok(c + 2):
+            if ok(c + 2):
                 prep(c + 2, "ad", 0, 4)
                 prep(c + 2, "sq", 0, 4)
-            if ok(c):
-                lead = 1 if by_py(c, 1) else 0
-                sl = (2 * lead, 2 * lead + 1, 2 - 2 * lead, 3 - 2 * lead)
-                flip_right(c, sl[0])
-                flip_right(c, sl[1])
+            lead = 1 if by_py(c, 1) and not by_py(c, 0) else 0
+            sl = (2 * lead, 2 * lead + 1, 2 - 2 * lead, 3 - 2 * lead)
+            flip_right(c, sl[0])
+            flip_right(c, sl[1])
             if ok(c - 1):
                 multiply(c - 1, 0)
-            if ok(c):
-                flip_right(c, sl[2])
-                if c > 0:
-                    left_side(c)
+            flip_right(c, sl[2])
+            if by_py(c, 0):
+                second_left(c, 0)
+            else:
+                left_side(c)
+            if by_py(c, 0):
+                second_left(c, 1)
             if c == CHUNKS - 1:
                 add_on_pool(c - 1, 0)
-            if ok(c + 2) and c >= 1:
-                prep(c + 2, "ng", 0, 4)
-                prep(c + 2, "nq", 0, 4)
-            if c == 0:
-                products(c, sl[0])
-                flip_right(c, sl[3])
             if ok(c + 1):
-                flip_copy(c + 1, FIRST)
-            if c == 0:
-                prep(1, "nq", 0, 4)
-            if ok(c + 2) and c >= 1:
-                prep(c + 2, "m1", 0, 4)
-            if ok(c) and c > 0:
-                products(c, sl[0])
-                flip_right(c, sl[3])
+                flip_gate(c + 1, 0)
+            if ok(c + 1):
+                flip_grad(c + 1, 0)
+                copy_grad(c + 1, 0)
+            if ok(c + 2):
+                prep(c + 2, "ng", 0, 4)
+            products(c, sl[0])
+            flip_right(c, sl[3])
             if ok(c - 1):
                 multiply(c - 1, 1)
             if ok(c + 1):
-                flip_copy(c + 1, 1 - FIRST)
-            if c == 0:
-                prep(1, "m1", 0, 4)
-            if ok(c):
-                for s in sl[1:4]:
-                    if s == sl[3] and c == CHUNKS - 1:
-                        quantise(c, sl[0], sl[0] + GROUP)
-                    products(c, s)
-            if c == 0:
-                difference_v(1)
-                nc.vector.quantize_mx(out=w_codes[:, N_PASS : N_PASS + D].bitcast(E4M3X4), scales=w_scales[:, N_PASS : N_PASS + D], in_=w_grouped[:])
-                if ADMIN <= 2:
-                    prep(2, "ad", 0, 4)
-                prep(2, "sq", 0, 4)
-                if zn(2):
-                    prep(2, "nq", 0, 4)
-                prep(2, "m1", 0, 4)
+                flip_gate(c + 1, 1)
+            if ok(c + 1):
+                flip_grad(c + 1, 1)
+                copy_grad(c + 1, 1)
+            if ok(c + 2):
+                prep(c + 2, "nq", 0, 4)
+            if ok(c + 2):
+                prep(c + 2, "m1", 0, 4)
+            products(c, sl[1])
+            products(c, sl[2])
+            if c == CHUNKS - 1:
+                quantise(c, sl[0], sl[0] + GROUP)
+            products(c, sl[3])
 
         w_rows = const.tile([P, D // P, K], BF16)
         load_first()
@@ -406,6 +396,7 @@ def tile_scan_pb_t_v_kernel(
         nc.sync.dma_start(out=w_rows[:, :, D:K], in_=w_gate[0:D, :].rearrange("(h r) k -> r h k", r=P))
         load(1)
         load(2)
+        load(3)
         ident = const.tile([P, P], F32)
         make_identity(nc, ident[:])
         w_codes = const.tile([P, N_PASS + D + D], U32, align_bytes=64)
@@ -418,23 +409,39 @@ def tile_scan_pb_t_v_kernel(
         prep(0, "sq", 0, 2)
         difference(0)
         first_left(0, 0)
-        vminus(0, 0, 2)
         second_left(0, 0)
+        vminus(0, 0, 2)
         flip_grad(0, 1)
         copy_grad(0, 1)
         flip_gate(0, 1)
         prep(0, "sq", 2, 4)
         prep(0, "m1", 2, 4)
+        first_left(0, 1)
+        second_left(0, 1)
+        direct_term(0)
+        flip_right(0, 0)
+        flip_right(0, 1)
+        flip_right(0, 2)
+        products(0, 0)
+        flip_right(0, 3)
+        prep(1, "sq", 0, 4)
         w_bank = sums.tile([P, 2, D], F32, tag="acc")
         for b in range(2):
             for half in range(D // P):
                 nc.tensor.transpose(w_bank[:, b, half * P : (half + 1) * P], w_rows[:, half, b * D : (b + 1) * D].bitcast(F32), ident[:])
         w_grouped = const.tile([P, D * PACK], BF16, align_bytes=64)
         nc.scalar.copy(out=w_grouped[:].bitcast(F32).rearrange("w (o b) -> w o b", b=2), in_=w_bank[:].rearrange("w b o -> w o b"))
-        first_left(0, 1)
-        second_left(0, 1)
-        direct_term(0)
-        for c in range(CHUNKS):
+        flip_copy(1, 0)
+        prep(1, "m1", 0, 4)
+        for s in (1, 2, 3):
+            products(0, s)
+        difference_v(1)
+        nc.vector.quantize_mx(out=w_codes[:, N_PASS : N_PASS + D].bitcast(E4M3X4), scales=w_scales[:, N_PASS : N_PASS + D], in_=w_grouped[:])
+        flip_copy(1, 1)
+        prep(2, "sq", 0, 4)
+        prep(2, "nq", 0, 4)
+        prep(2, "m1", 0, 4)
+        for c in range(1, CHUNKS):
             step(c)
         last = CHUNKS - 1
         multiply(last, 1)

from contextlib import ExitStack

import concourse.mybir as mybir
from concourse.masks import make_identity

F32 = mybir.dt.float32
BF16 = mybir.dt.bfloat16
U32 = mybir.dt.uint32
U8 = mybir.dt.uint8
I32 = mybir.dt.int32
E5M2X4 = mybir.dt.float8_e5m2_x4
E4M3X4 = mybir.dt.float8_e4m3fn_x4
ALU = mybir.AluOpType
ACT = mybir.ActivationFunctionType

P = 128
D = 256
K = 2 * D
PACK = 4
PAIR = 2
TOKENS = 8 * 8 * 128
PER_PARTITION = TOKENS // P
SLOTS = 4
CHUNKS = PER_PARTITION // SLOTS
GROUP = 2
GROUPS_PER_CHUNK = SLOTS // GROUP
COLS = GROUP * P
N_PASS = 512
AHEAD = 3
TBUFS = 3
ADMIN = 99
PYMIN = 3

FIRST = 0
FLOPS = 2 * TOKENS * K * D
BYTES = TOKENS * D * (2 + 4 + 4 + 2 + 4) + 2 * D * D * 2


def by_partition(dram):
    return dram.flatten_outer_dims().rearrange("(p n) d -> p n d", n=PER_PARTITION)


def tile_scan_pb_t_v_kernel(
    tc, query, wc, w_lin, b_lin, w_gate, b_gate, upd, gate, grad_out, out
):
    nc = tc.nc
    query_v, upd_v, gate_v, grad_v, out_v = (
        by_partition(x) for x in (query, upd, gate, grad_out, out)
    )

    with ExitStack() as stack:
        const = stack.enter_context(tc.tile_pool(name="const", bufs=1))
        inputs = stack.enter_context(tc.tile_pool(name="inputs", bufs=5))
        prepared = stack.enter_context(tc.tile_pool(name="prepared", bufs=4))
        factors = stack.enter_context(tc.tile_pool(name="factors", bufs=3))
        packed = stack.enter_context(tc.tile_pool(name="packed", bufs=3))
        direct = stack.enter_context(tc.tile_pool(name="direct", bufs=TBUFS))
        gate_banks = stack.enter_context(tc.psum_pool(name="gate_banks", bufs=2))
        grad_banks = stack.enter_context(tc.psum_pool(name="grad_banks", bufs=1))
        right_banks = stack.enter_context(tc.psum_pool(name="right_banks", bufs=3))
        sums = stack.enter_context(tc.psum_pool(name="sums", bufs=2))
        stack.enter_context(tc.manual_schedule())
        negq = stack.enter_context(tc.tile_pool(name="negq", bufs=2))
        diffs = stack.enter_context(tc.tile_pool(name="diffs", bufs=2))
        results = stack.enter_context(tc.tile_pool(name="results", bufs=4))
        chunk = {}

        def load(c):
            gate_in = inputs.tile([P, SLOTS, D], F32)
            grad_in = inputs.tile([P, SLOTS, D], BF16)
            upd_in = inputs.tile([P, SLOTS, D], F32)
            query_in = inputs.tile([P, SLOTS, D], BF16)
            parts = ((0, 2), (2, 4)) if c < 1 else ((0, 4),)
            for pair in (((upd_in, upd_v), (query_in, query_v)), ((grad_in, grad_v), (gate_in, gate_v))):
                for lo, hi in parts:
                    for t, v in pair:
                        nc.sync.dma_start(out=t[:, lo:hi, :], in_=v[:, c * SLOTS + lo : c * SLOTS + hi, :])
            chunk[c] = {"gate": gate_in, "grad": grad_in, "upd": upd_in, "query": query_in}

        def load_piece(c, lo, hi):
            m = chunk[c]
            for name, v in (("grad", grad_v), ("gate", gate_v), ("upd", upd_v), ("query", query_v)):
                nc.sync.dma_start(out=m[name][:, lo:hi, :], in_=v[:, c * SLOTS + lo : c * SLOTS + hi, :])

        def load_first():
            gate_in = inputs.tile([P, SLOTS, D], F32)
            grad_in = inputs.tile([P, SLOTS, D], BF16)
            upd_in = inputs.tile([P, SLOTS, D], F32)
            query_in = inputs.tile([P, SLOTS, D], BF16)
            chunk[0] = {"gate": gate_in, "grad": grad_in, "upd": upd_in, "query": query_in}
            load_piece(0, 0, 2)

        def load_second():
            load_piece(0, 2, 4)

        def vminus(c, lo, hi):
            sq = chunk[c]["upd_sq"][:, lo:hi]
            nc.vector.tensor_scalar(out=sq, in0=sq, scalar1=-1.0, scalar2=None, op0=ALU.add)

        def pieces(c):
            return ((0, 2), (2, 4)) if c < 1 else ((0, 4),)

        def de(ap):
            return ap.rearrange("r s (w e) -> r s e w", e=PAIR)

        def zn(c):
            return {2: 2}.get(c, 1 if c > 3 else 0)

        def by_py(c, h):
            return c >= PYMIN and (h == 1 or 2 < c < CHUNKS - 1)

        def prep(c, what, lo, hi):
            m = chunk[c]
            sl = slice(lo, hi)
            if what == "sq":
                if lo == 0:
                    upd_sq = prepared.tile([P, SLOTS, PAIR, P], F32)
                    m["upd_sq"] = upd_sq
                nc.scalar.activation(out=m["upd_sq"][:, sl], in_=de(m["upd"][:, sl, :]), func=ACT.Square)
            elif what == "ng":
                if any(by_py(c, h) for h in range(2)):
                    neg_grad = prepared.tile([P, SLOTS, PAIR, P], F32)
                    m["neg_grad"] = neg_grad
                    for h in range(2):
                        if by_py(c, h):
                            nc.scalar.activation(out=neg_grad[:, 2 * h : 2 * h + 2], in_=de(m["grad"][:, 2 * h : 2 * h + 2, :]), func=ACT.Copy, scale=-1.0)
            elif what == "nq":
                k = zn(c)
                if k == 0:
                    return
                neg_query = negq.tile([P, SLOTS, PAIR, P], F32)
                m["neg_query"] = neg_query
                nc.scalar.activation(out=neg_query[:, 0:k], in_=de(m["query"][:, 0:k, :]), func=ACT.Copy, scale=-1.0)
            elif what == "ad":
                if c < ADMIN:
                    return
                if lo == 0:
                    gate_de = prepared.tile([P, SLOTS, PAIR, P], F32)
                    m["gate_de"] = gate_de
                nc.scalar.copy(out=m["gate_de"][:, sl], in_=de(m["gate"][:, sl, :]))
            else:
                nc.scalar.activation(out=m["upd_sq"][:, sl], in_=m["upd_sq"][:, sl], func=ACT.Copy, bias=-1.0, scale=1.0)

        def flip_grad(c, h):
            m = chunk[c]
            if by_py(c, h):
                neg_gb = grad_banks.tile([P, PAIR, COLS], F32, tag="grad_words")
                for s in range(GROUP):
                    for e in range(PAIR):
                        o = neg_gb[:, e, s * P : (s + 1) * P]
                        nc.tensor.matmul(out=o, lhsT=m["ga"][:, h * GROUP + s, e, :], rhs=ident[:], start=True, stop=False, is_transpose=True)
                        nc.tensor.matmul(out=o, lhsT=m["neg_grad"][:, h * GROUP + s, e, :], rhs=ident[:], start=False, stop=True, is_transpose=True)
                m["neg_gb", h] = neg_gb
            else:
                grad_words = grad_banks.tile([P, COLS], F32)
                for s in range(GROUP):
                    nc.tensor.transpose(grad_words[:, s * P : (s + 1) * P], m["grad"][:, h * GROUP + s, :].bitcast(F32), ident[:])
                m["grad_words", h] = grad_words

        def flip_gate(c, h):
            m = chunk[c]
            gate_t = gate_banks.tile([P, PAIR, COLS], F32)
            for s in range(GROUP):
                for e in range(PAIR):
                    if c >= ADMIN:
                        src = m["gate_de"][:, h * GROUP + s, e, :]
                    else:
                        src = m["gate"][:, h * GROUP + s, :].rearrange("r (w e) -> r e w", e=PAIR)[:, e, :]
                    nc.tensor.transpose(gate_t[:, e, s * P : (s + 1) * P], src, ident[:])
            m["gate_t", h] = gate_t[:].rearrange("w e n -> w n e")

        def copy_grad(c, h):
            m = chunk[c]
            if "left" not in m:
                left = factors.tile([P, 2, SLOTS * P, PAIR], F32)
                m["left"] = left
            if by_py(c, h):
                nc.scalar.copy(out=m["left"][:, 0, h * COLS : (h + 1) * COLS, :], in_=m["neg_gb", h][:].rearrange("w e n -> w n e"))
            else:
                grad_sb = factors.tile([P, COLS], F32)
                nc.scalar.copy(out=grad_sb[:], in_=m["grad_words", h][:])
                m["grad_t", h] = grad_sb[:].bitcast(BF16).rearrange("w (n e) -> w n e", e=PAIR)

        def flip_right(c, s):
            m = chunk[c]
            right = right_banks.tile([P, 2, PAIR, P], F32)
            for e in range(PAIR):
                nc.tensor.transpose(right[:, 0, e, :], m["upd_sq"][:, s, e, :], ident[:])
            for e in range(PAIR):
                if s < zn(c):
                    ue = m["upd"][:, s, :].rearrange("r (w e) -> r e w", e=PAIR)
                    nc.tensor.matmul(out=right[:, 1, e, :], lhsT=ue[:, e, :], rhs=ident[:], start=True, stop=False, is_transpose=True)
                    nc.tensor.matmul(out=right[:, 1, e, :], lhsT=m["neg_query"][:, s, e, :], rhs=ident[:], start=False, stop=True, is_transpose=True)
                else:
                    nc.tensor.transpose(right[:, 1, e, :], m["diff"][:, s, e, :], ident[:])
            m["right", s] = right

        def first_left(c, h):
            m = chunk[c]
            cs = slice(h * COLS, (h + 1) * COLS)
            if not by_py(c, h):
                nc.vector.scalar_tensor_tensor(out=m["left"][:, 0, cs, :], in0=m["gate_t", h], scalar=1.0, in1=m["grad_t", h], op0=ALU.subtract, op1=ALU.mult)

        def second_left(c, h):
            m = chunk[c]
            cs = slice(h * COLS, (h + 1) * COLS)
            nc.vector.tensor_tensor(out=m["left"][:, 1, cs, :], in0=m["gate_t", h], in1=m["left"][:, 0, cs, :], op=ALU.mult)

        def direct_term(c):
            m = chunk[c]
            if "ga" not in m:
                ga = direct.tile([P, SLOTS, PAIR, P], F32)
                m["ga"] = ga
            ga = m["ga"]
            for lo, hi in ((0, 2), (2, 4)) if by_py(c, 0) else ((0, 4),):
                src = m["gate_de"][:, lo:hi] if c >= ADMIN else de(m["gate"][:, lo:hi, :])
                nc.gpsimd.tensor_tensor(out=ga[:, lo:hi], in0=de(m["grad"][:, lo:hi, :]), in1=src, op=ALU.mult)

        def difference(c):
            m = chunk[c]
            diff = diffs.tile([P, SLOTS, PAIR, P], F32)
            for lo, hi in pieces(c):
                lo = max(lo, zn(c))
                nc.gpsimd.tensor_tensor(out=diff[:, lo:hi], in0=de(m["upd"][:, lo:hi, :]), in1=de(m["query"][:, lo:hi, :]), op=ALU.subtract)
            m["diff"] = diff

        def difference_v(c):
            m = chunk[c]
            diff = diffs.tile([P, SLOTS, PAIR, P], F32)
            for lo, hi in ((0, 2), (2, 4)):
                nc.vector.tensor_tensor(out=diff[:, lo:hi], in0=de(m["upd"][:, lo:hi, :]), in1=de(m["query"][:, lo:hi, :]), op=ALU.subtract)
            m["diff"] = diff

        def products(c, s):
            m = chunk[c]
            if "grouped" not in m:
                grouped = packed.tile([P, SLOTS * P, PACK], BF16, align_bytes=64)
                m["grouped"] = grouped
            cs = slice(s * P, (s + 1) * P)
            nc.vector.tensor_tensor(
                out=m["grouped"][:, cs, :].rearrange("w n (b e) -> w n b e", e=PAIR),
                in0=m["right", s][:].rearrange("w b e n -> w n b e"),
                in1=m["left"][:, :, cs, :].rearrange("w b n e -> w n b e"),
                op=ALU.mult,
            )

        def quantise(c, lo=0, hi=SLOTS):
            m = chunk[c]
            if "codes" not in m:
                dz_codes = packed.tile([P, SLOTS * P], U32, align_bytes=64)
                dz_scales = packed.tile([P, SLOTS * P], U8, align_bytes=64)
                m["codes"] = dz_codes
                m["scales"] = dz_scales
            cols = slice(lo * P, hi * P)
            nc.vector.quantize_mx(
                out=m["codes"][:, cols].bitcast(E5M2X4),
                scales=m["scales"][:, cols],
                in_=m["grouped"][:, cols, :].rearrange("w n t -> w (n t)"),
            )

        def mx_pass(c, h, i, n):
            m = chunk[c]
            if i == 0:
                if c == CHUNKS - 1:
                    acc = right_banks.tile([P, GROUP, D], F32, tag="right")
                else:
                    acc = sums.tile([P, GROUP, D], F32, tag="acc")
                m["acc", h] = acc
            s = 2 * h + min(i, 1)
            tokens = slice(s * P, (s + 1) * P)
            w0 = (N_PASS, D, 0, 0, 0, 0)[i]
            nc.tensor.matmul_mx(
                out=m["acc", h][:].rearrange("r s o -> r (s o)"),
                lhsT=m["codes"][:, tokens].bitcast(E5M2X4), lhsT_scale=m["scales"][:, tokens],
                rhs=w_codes[:, w0 : w0 + N_PASS].bitcast(E4M3X4), rhs_scale=w_scales[:, w0 : w0 + N_PASS],
                start=(i == 0), stop=(i == n - 1),
            )

        def multiply(c, h):
            for i in range(2):
                mx_pass(c, h, i, 2)

        def add_and_store(c, h, step=GROUP):
            m = chunk[c]
            result = results.tile([P, GROUP, D], F32)
            for lo in range(0, GROUP, step):
                part = slice(lo, lo + step)
                slots = slice(h * GROUP + lo, h * GROUP + lo + step)
                nc.vector.tensor_tensor(
                    out=result[:, part].rearrange("r s (w e) -> r s w e", e=PAIR),
                    in0=m["acc", h][:, part].rearrange("r s (w e) -> r s w e", e=PAIR),
                    in1=m["ga"][:, slots].rearrange("r s e w -> r s w e"), op=ALU.add)
                nc.sync.dma_start(out=out_v[:, c * SLOTS + slots.start : c * SLOTS + slots.stop, :], in_=result[:, part])

        def add_on_pool(c, h):
            m = chunk[c]
            result = results.tile([P, GROUP, D], F32)
            nc.scalar.copy(out=result[:], in_=m["acc", h][:])
            words = result[:].rearrange("r s (w e) -> r s w e", e=PAIR)
            nc.gpsimd.tensor_tensor(
                out=words, in0=words,
                in1=m["ga"][:, h * GROUP : (h + 1) * GROUP].rearrange("r s e w -> r s w e"), op=ALU.add)
            nc.sync.dma_start(out=out_v[:, c * SLOTS + h * GROUP : c * SLOTS + (h + 1) * GROUP, :], in_=result[:])

        ok = lambda x: 0 <= x < CHUNKS

        def scalar_prep(c):
            for lo, hi in pieces(c):
                if c >= ADMIN:
                    prep(c, "ad", lo, hi)
                prep(c, "sq", lo, hi)
                if lo == 0:
                    prep(c, "ng", 0, 4)
                prep(c, "m1", lo, hi)

        def left_side(c):
            m = chunk[c]
            lead = 1 if by_py(c, 1) and not by_py(c, 0) else 0
            m["order"] = (lead, 1 - lead)
            for h in range(2):
                if not by_py(c, h):
                    first_left(c, h)
            for h in m["order"]:
                second_left(c, h)

        def flip_copy(c, h):
            flip_gate(c, h)
            flip_grad(c, h)
            copy_grad(c, h)

        def step(c):
            if ok(c + AHEAD):
                load(c + AHEAD)
            if ok(c - 2):
                add_and_store(c - 2, 0)
            if ok(c - 2):
                add_and_store(c - 2, 1)
            if ok(c - 1):
                quantise(c - 1)
            if ok(c + 1):
                for j in (1, 2) if c == 1 else (c + 1,):
                    ga = direct.tile([P, SLOTS, PAIR, P], F32)
                    chunk[j]["ga"] = ga
                    if c == 1:
                        nc.vector.memset(ga[:, 0, 0, 0:1], 0.0)
                    direct_term(j)
                difference(c + 1)
            if ok(c + 2):
                prep(c + 2, "ad", 0, 4)
                prep(c + 2, "sq", 0, 4)
            lead = 1 if by_py(c, 1) and not by_py(c, 0) else 0
            sl = (2 * lead, 2 * lead + 1, 2 - 2 * lead, 3 - 2 * lead)
            flip_right(c, sl[0])
            flip_right(c, sl[1])
            if ok(c - 1):
                multiply(c - 1, 0)
            flip_right(c, sl[2])
            if by_py(c, 0):
                second_left(c, 0)
            else:
                left_side(c)
            if by_py(c, 0):
                second_left(c, 1)
            if c == CHUNKS - 1:
                add_on_pool(c - 1, 0)
            if ok(c + 1):
                flip_gate(c + 1, 0)
            if ok(c + 1):
                flip_grad(c + 1, 0)
                copy_grad(c + 1, 0)
            if ok(c + 2):
                prep(c + 2, "ng", 0, 4)
            products(c, sl[0])
            flip_right(c, sl[3])
            if ok(c - 1):
                multiply(c - 1, 1)
            if ok(c + 1):
                flip_gate(c + 1, 1)
            if ok(c + 1):
                flip_grad(c + 1, 1)
                copy_grad(c + 1, 1)
            if ok(c + 2):
                prep(c + 2, "nq", 0, 4)
            if ok(c + 2):
                prep(c + 2, "m1", 0, 4)
            products(c, sl[1])
            products(c, sl[2])
            if c == CHUNKS - 1:
                quantise(c, sl[0], sl[0] + GROUP)
            products(c, sl[3])

        w_rows = const.tile([P, D // P, K], BF16)
        load_first()
        load_second()
        nc.sync.dma_start(out=w_rows[:, :, 0:D], in_=w_lin[0:D, :].rearrange("(h r) k -> r h k", r=P))
        nc.sync.dma_start(out=w_rows[:, :, D:K], in_=w_gate[0:D, :].rearrange("(h r) k -> r h k", r=P))
        load(1)
        load(2)
        load(3)
        ident = const.tile([P, P], F32)
        make_identity(nc, ident[:])
        w_codes = const.tile([P, N_PASS + D + D], U32, align_bytes=64)
        w_scales = const.tile([P, N_PASS + D + D], U8, align_bytes=64)
        nc.vector.memset(w_codes[:].bitcast(I32), 0)
        nc.vector.memset(w_scales[:].bitcast(I32), 0)
        flip_grad(0, 0)
        copy_grad(0, 0)
        flip_gate(0, 0)
        prep(0, "sq", 0, 2)
        difference(0)
        first_left(0, 0)
        second_left(0, 0)
        vminus(0, 0, 2)
        flip_grad(0, 1)
        copy_grad(0, 1)
        flip_gate(0, 1)
        prep(0, "sq", 2, 4)
        prep(0, "m1", 2, 4)
        first_left(0, 1)
        second_left(0, 1)
        direct_term(0)
        flip_right(0, 0)
        flip_right(0, 1)
        flip_right(0, 2)
        products(0, 0)
        flip_right(0, 3)
        prep(1, "sq", 0, 4)
        w_bank = sums.tile([P, 2, D], F32, tag="acc")
        for b in range(2):
            for half in range(D // P):
                nc.tensor.transpose(w_bank[:, b, half * P : (half + 1) * P], w_rows[:, half, b * D : (b + 1) * D].bitcast(F32), ident[:])
        w_grouped = const.tile([P, D * PACK], BF16, align_bytes=64)
        nc.scalar.copy(out=w_grouped[:].bitcast(F32).rearrange("w (o b) -> w o b", b=2), in_=w_bank[:].rearrange("w b o -> w o b"))
        flip_copy(1, 0)
        prep(1, "m1", 0, 4)
        for s in (1, 2, 3):
            products(0, s)
        difference_v(1)
        nc.vector.quantize_mx(out=w_codes[:, N_PASS : N_PASS + D].bitcast(E4M3X4), scales=w_scales[:, N_PASS : N_PASS + D], in_=w_grouped[:])
        flip_copy(1, 1)
        prep(2, "sq", 0, 4)
        prep(2, "nq", 0, 4)
        prep(2, "m1", 0, 4)
        for c in range(1, CHUNKS):
            step(c)
        last = CHUNKS - 1
        multiply(last, 1)
        quantise(last, 0, GROUP)
        multiply(last, 0)
        add_and_store(last - 1, 1)
        add_and_store(last, 1)
        add_and_store(last, 0, 1)
